import numpy as np
import ml_dtypes


def mxq(x, axis, fmt="e4m3"):
    dtype, down = {"e4m3": (ml_dtypes.float8_e4m3fn, 7), "e5m2": (ml_dtypes.float8_e5m2, 14)}[fmt]
    v = np.moveaxis(np.asarray(x, np.float32).astype(ml_dtypes.bfloat16).astype(np.float64), axis, -1)
    blocks = v.reshape(v.shape[:-1] + (-1, 32))
    amax = np.abs(blocks).max(-1, keepdims=True)
    byte = np.maximum(np.where(amax > 0, np.frexp(amax)[1] - 1 + 127, 0) - down, 1)
    scale = np.exp2(byte - 127.0)
    codes = (blocks / scale).astype(np.float32).astype(dtype).astype(np.float64)
    return np.moveaxis((codes * scale).reshape(v.shape), -1, axis)


WIDE = False


def mx_kscale(k):
    if not WIDE:
        return np.ones(k)
    levels = np.array([10, -10, 5, -5, 0])
    a = np.random.permutation(np.resize(levels, k // 512 * 4)).reshape(k // 512, 4)
    idx = np.arange(k)
    return np.exp2(a[idx // 512, idx % 128 // 32])


BF16 = ml_dtypes.bfloat16


def bf(x):
    return np.asarray(x, np.float32).astype(BF16)


def f64(x):
    return np.asarray(x).astype(np.float64)


E2M1 = np.array([0.0, 0.5, 1.0, 1.5, 2.0, 3.0, 4.0, 6.0, -0.0, -0.5, -1.0, -1.5, -2.0, -3.0, -4.0, -6.0])


def pack_weight(w, fmt):
    k, n = w.shape
    w = f64(bf(w)).reshape(k // 32, 32, n)
    amax = np.abs(w).max(1)
    if fmt == "e4m3":
        byte = np.frexp(amax)[1] - 1 + 127 - 7
    else:
        mant, ex = np.frexp(amax / 6.0)
        byte = np.where(mant > 0.5, ex, ex - 1) + 127
    byte = np.clip(np.where(amax > 0, byte, 1), 1, 254)
    scaled = (w * np.exp2(127.0 - byte)[:, None, :]).reshape(k, n).astype(np.float32)
    by_word = np.ascontiguousarray(scaled.reshape(k // 512, 128, 4, n).transpose(0, 1, 3, 2))
    if fmt == "e4m3":
        words = by_word.astype(ml_dtypes.float8_e4m3fn).view(np.uint8)
    else:
        c = by_word.astype(ml_dtypes.float4_e2m1fn).view(np.uint8) & 0xF
        words = c[..., 0::2] | (c[..., 1::2] << 4)
    return np.ascontiguousarray(words), np.ascontiguousarray(byte.astype(np.uint8).reshape(k // 512, 16, n))


def unpack_weight(words, scales, fmt):
    g, p, n, _ = words.shape
    if fmt == "e4m3":
        vals = np.ascontiguousarray(words).view(ml_dtypes.float8_e4m3fn).astype(np.float64)
    else:
        nib = np.empty((g, p, n, 4), np.uint8)
        nib[..., 0::2] = words & 0xF
        nib[..., 1::2] = words >> 4
        vals = E2M1[nib]
    vals = vals * np.repeat(np.exp2(scales.astype(np.float64) - 127.0), 8, axis=1)[..., None]
    return vals.transpose(0, 1, 3, 2).reshape(g * 512, n)

def pack4(w):
    words, scales = pack_weight(w, "e2m1")
    return words.reshape(words.shape[0], 128, -1), scales


def unpack4(words, scales):
    return unpack_weight(words.reshape(words.shape[0], 128, -1, 2), scales, "e2m1")


B, I, O, G = 1280, 512, 128, 2
K = I * G


def bspline_basis(d):
    inner = 1.0 - 6.0 * d * d + 6.0 * d * d * d
    outer = 2.0 * (1.0 - d) ** 3
    return np.where(d < 0.5, inner, np.where(d < 1.0, outer, np.zeros_like(d)))


def setup_inputs():
    g = np.linspace(-1.0, 1.0, G)
    s = mx_kscale(I)
    u = s / s.max()
    x_norm = bf(np.tanh(np.random.standard_normal((B, I))) * u)
    spline_weight = bf(np.random.standard_normal((O, I, G)) / np.sqrt(I))
    base_activation = np.random.standard_normal((O, I)) * 4.0 / np.sqrt(I) / u
    words, scales = pack4(base_activation.T)
    grid_points = bf(g + 0.1 * (g[1] - g[0]) * np.random.standard_normal(G))
    return {"x_norm": x_norm,
            "spline_weight": spline_weight,
            "base_activation_words": words,
            "base_activation_scales": scales,
            "grid_points": grid_points}


def reference(x_norm, spline_weight, base_activation_words, base_activation_scales, grid_points):
    t = f64(x_norm)
    d = np.abs(t[:, :, None] - f64(grid_points))
    basis = bspline_basis(d)
    spline_out = mxq(basis.reshape(B, K), 1, "e4m3") @ mxq(f64(spline_weight).reshape(O, K), 1, "e4m3").T
    base_out = mxq(t, 1, "e4m3") @ unpack4(base_activation_words, base_activation_scales)
    return spline_out + 0.1 * base_out

@@ -1,0 +1,193 @@
+from contextlib import ExitStack
+
+import concourse.mybir as mybir
+from concourse.masks import make_identity
+
+F32 = mybir.dt.float32
+BF16 = mybir.dt.bfloat16
+I32 = mybir.dt.int32
+U32 = mybir.dt.uint32
+U8 = mybir.dt.uint8
+FP8X4 = mybir.dt.float8_e4m3fn_x4
+FP4X4 = mybir.dt.float4_e2m1fn_x4
+ACT = mybir.ActivationFunctionType
+ALU = mybir.AluOpType
+
+P = 128
+PACK = 4
+BATCH, FEATURES, OUTPUTS, GRID = 1280, 512, 128, 2
+ROW_TILES = BATCH // P
+TILES_PER_CHUNK = 2
+CHUNKS = ROW_TILES // TILES_PER_CHUNK
+CHUNK_ROWS = TILES_PER_CHUNK * P
+HALVES = 2
+PAIR = 2
+CHUNK_X = HALVES * CHUNK_ROWS * PAIR
+
+FLOPS = 2 * BATCH * OUTPUTS * (FEATURES * GRID + FEATURES)
+
+
+def tile_advancedkanlayer_pa_s_kernel(
+    tc, x_norm, spline_weight, base_activation_words, base_activation_scales, grid_points, out
+):
+    nc = tc.nc
+    x_rows = x_norm.rearrange("(p r) i -> p r i", r=ROW_TILES)
+    out_rows = out.rearrange("(p r) o -> p r o", r=ROW_TILES)
+
+    with ExitStack() as stack:
+        consts = stack.enter_context(tc.tile_pool(name="consts", bufs=1))
+        loads = stack.enter_context(tc.tile_pool(name="loads", bufs=CHUNKS))
+        work = stack.enter_context(tc.tile_pool(name="work", bufs=3))
+        psum_w = stack.enter_context(tc.psum_pool(name="psum_w", bufs=1))
+        psum_x = stack.enter_context(tc.psum_pool(name="psum_x", bufs=4))
+        psum_out = stack.enter_context(tc.psum_pool(name="psum_out", bufs=2))
+
+        grid_bf = consts.tile([P, GRID], BF16)
+        nc.scalar.dma_start(out=grid_bf[:], in_=grid_points.partition_broadcast(P))
+        spline_sb = consts.tile([P, FEATURES * GRID], BF16)
+        nc.scalar.dma_start(out=spline_sb[:], in_=spline_weight.rearrange("o i g -> o (i g)"))
+
+        x_chunks = []
+        for c in range(CHUNKS):
+            x_sb = loads.tile([P, TILES_PER_CHUNK, FEATURES], BF16)
+            nc.sync.dma_start(
+                out=x_sb[:], in_=x_rows[:, c * TILES_PER_CHUNK : (c + 1) * TILES_PER_CHUNK, :]
+            )
+            x_chunks.append(x_sb)
+
+        base_words = consts.tile([P, 2 * OUTPUTS], U8, align_bytes=64)
+        base_scales = consts.tile([P, OUTPUTS], U8, align_bytes=64)
+        nc.vector.memset(base_scales[:].bitcast(I32), 0)
+        nc.sync.dma_start(out=base_words[:].bitcast(I32), in_=base_activation_words[0].bitcast(I32))
+        for quadrant in range(4):
+            nc.sync.dma_start(
+                out=base_scales[32 * quadrant : 32 * quadrant + 4, :].bitcast(I32),
+                in_=base_activation_scales[0, 4 * quadrant : 4 * quadrant + 4, :].bitcast(I32),
+            )
+
+        identity = consts.tile([P, P], F32)
+        make_identity(nc, identity[:])
+
+        minus_grid = consts.tile([P, GRID], F32)
+        nc.vector.tensor_scalar_mul(out=minus_grid[:], in0=grid_bf[:], scalar1=-1.0)
+        minus_twice_grid = consts.tile([P, GRID], F32)
+        nc.vector.tensor_scalar_mul(out=minus_twice_grid[:], in0=grid_bf[:], scalar1=-2.0)
+
+        spline_sorted = consts.tile([P, PACK, P], F32)
+        nc.vector.tensor_copy(
+            out=spline_sorted[:], in_=spline_sb[:].bitcast(F32).rearrange("o (p j) -> o j p", j=PACK)
+        )
+        spline_t = psum_w.tile([P, PACK, OUTPUTS], F32)
+        for j in range(PACK):
+            nc.tensor.transpose(spline_t[:, j, :], spline_sorted[:, j, :], identity[:])
+        spline_grouped = consts.tile([P, HALVES, OUTPUTS, PACK], BF16, align_bytes=64)
+        nc.vector.tensor_copy(
+            out=spline_grouped[:].bitcast(F32),
+            in_=spline_t[:].rearrange("p (u e) o -> p u o e", u=HALVES),
+        )
+        spline_codes = consts.tile([P, HALVES, OUTPUTS], U32, align_bytes=64)
+        spline_scales = consts.tile([P, HALVES, OUTPUTS], U8, align_bytes=64)
+        nc.vector.quantize_mx(
+            out=spline_codes[:].rearrange("p u o -> p (u o)").bitcast(FP8X4),
+            scales=spline_scales[:].rearrange("p u o -> p (u o)"),
+            in_=spline_grouped[:].rearrange("p u o t -> p (u o t)"),
+        )
+
+        for c in range(CHUNKS):
+            x_sb = x_chunks[c]
+            x_t = psum_x.tile([P, HALVES, CHUNK_ROWS], F32)
+            for r in range(TILES_PER_CHUNK):
+                x_words = x_sb[:, r, :].bitcast(F32)
+                for u in range(HALVES):
+                    nc.tensor.transpose(
+                        x_t[:, u, r * P : (r + 1) * P],
+                        x_words[:, u : FEATURES // PAIR : HALVES],
+                        identity[:],
+                    )
+            x_values = x_t[:].rearrange("p u n -> p (u n)").bitcast(BF16)
+
+            x_grouped = work.tile([P, CHUNK_ROWS, PACK], BF16, align_bytes=64)
+            nc.scalar.copy(out=x_grouped[:].bitcast(F32), in_=x_t[:].rearrange("p u n -> p n u"))
+
+            twice_dist = work.tile([P, GRID, CHUNK_X], F32)
+            dist_sq = work.tile([P, GRID, CHUNK_X], F32)
+            gap_sq = work.tile([P, GRID, CHUNK_X], F32)
+            for g in range(GRID):
+                nc.scalar.activation(
+                    out=twice_dist[:, g, :], in_=x_values, func=ACT.Abs,
+                    bias=minus_twice_grid[:, g : g + 1], scale=2.0,
+                )
+            for g in range(GRID):
+                nc.scalar.activation(
+                    out=dist_sq[:, g, :], in_=x_values, func=ACT.Square,
+                    bias=minus_grid[:, g : g + 1], scale=1.0,
+                )
+            nc.scalar.activation(out=gap_sq[:], in_=twice_dist[:], func=ACT.Square, bias=1.0, scale=-0.5)
+
+            twice_gap = work.tile([P, GRID, CHUNK_X], F32)
+            nc.vector.tensor_scalar(
+                out=twice_gap[:], in0=twice_dist[:], scalar1=-1.0, scalar2=2.0, op0=ALU.mult, op1=ALU.add
+            )
+            outer = work.tile([P, GRID, CHUNK_X], F32)
+            nc.vector.scalar_tensor_tensor(
+                out=outer[:], in0=twice_gap[:], scalar=0.0, in1=gap_sq[:], op0=ALU.max, op1=ALU.mult
+            )
+            inner_less_one = work.tile([P, GRID, CHUNK_X], F32)
+            nc.vector.scalar_tensor_tensor(
+                out=inner_less_one[:], in0=dist_sq[:], scalar=-3.0, in1=twice_gap[:],
+                op0=ALU.mult, op1=ALU.mult,
+            )
+            basis = work.tile([P, CHUNK_X, GRID], BF16, align_bytes=64)
+            nc.vector.scalar_tensor_tensor(
+                out=basis[:],
+                in0=inner_less_one[:].rearrange("p g n -> p n g"),
+                scalar=1.0,
+                in1=outer[:].rearrange("p g n -> p n g"),
+                op0=ALU.add,
+                op1=ALU.min,
+            )
+
+            basis_codes = work.tile([P, HALVES, TILES_PER_CHUNK, P], U32, align_bytes=64)
+            basis_scales = work.tile([P, HALVES, TILES_PER_CHUNK, P], U8, align_bytes=64)
+            nc.vector.quantize_mx(
+                out=basis_codes[:].rearrange("p u r b -> p (u r b)").bitcast(FP8X4),
+                scales=basis_scales[:].rearrange("p u r b -> p (u r b)"),
+                in_=basis[:].rearrange("p n g -> p (n g)"),
+            )
+            x_codes = work.tile([P, TILES_PER_CHUNK, P], U32, align_bytes=64)
+            x_scales = work.tile([P, TILES_PER_CHUNK, P], U8, align_bytes=64)
+            nc.vector.quantize_mx(
+                out=x_codes[:].rearrange("p r b -> p (r b)").bitcast(FP8X4),
+                scales=x_scales[:].rearrange("p r b -> p (r b)"),
+                in_=x_grouped[:].rearrange("p n t -> p (n t)"),
+            )
+
+            sums = psum_out.tile([P, TILES_PER_CHUNK, 2, OUTPUTS], F32)
+            for r in range(TILES_PER_CHUNK):
+                for u in range(HALVES):
+                    nc.tensor.matmul_mx(
+                        out=sums[:, r, 0, :],
+                        lhsT=basis_codes[:, u, r, :].bitcast(FP8X4),
+                        lhsT_scale=basis_scales[:, u, r, :],
+                        rhs=spline_codes[:, u, :].bitcast(FP8X4),
+                        rhs_scale=spline_scales[:, u, :],
+                        start=(u == 0),
+                        stop=(u == HALVES - 1),
+                    )
+                nc.tensor.matmul_mx(
+                    out=sums[:, r, 1, :],
+                    lhsT=x_codes[:, r, :].bitcast(FP8X4),
+                    lhsT_scale=x_scales[:, r, :],
+                    rhs=base_words[:].bitcast(FP4X4),
+                    rhs_scale=base_scales[:],
+                    start=True,
+                    stop=True,
+                )
+
+            tenth_base = work.tile([P, TILES_PER_CHUNK, OUTPUTS], F32)
+            nc.scalar.mul(out=tenth_base[:], in_=sums[:, :, 1, :], mul=0.1)
+            result = work.tile([P, TILES_PER_CHUNK, OUTPUTS], F32)
+            nc.vector.tensor_add(out=result[:], in0=sums[:, :, 0, :], in1=tenth_base[:])
+            nc.sync.dma_start(
+                out=out_rows[:, c * TILES_PER_CHUNK : (c + 1) * TILES_PER_CHUNK, :], in_=result[:]
+            )

@@ -39,8 +39,9 @@ def tile_advancedkanlayer_pa_s_kernel(
         loads = stack.enter_context(tc.tile_pool(name="loads", bufs=CHUNKS))
         work = stack.enter_context(tc.tile_pool(name="work", bufs=3))
         psum_w = stack.enter_context(tc.psum_pool(name="psum_w", bufs=1))
-        psum_x = stack.enter_context(tc.psum_pool(name="psum_x", bufs=4))
+        psum_x = stack.enter_context(tc.psum_pool(name="psum_x", bufs=CHUNKS))
         psum_out = stack.enter_context(tc.psum_pool(name="psum_out", bufs=2))
+        stack.enter_context(tc.manual_schedule())
 
         grid_bf = consts.tile([P, GRID], BF16)
         nc.scalar.dma_start(out=grid_bf[:], in_=grid_points.partition_broadcast(P))
@@ -68,10 +69,22 @@ def tile_advancedkanlayer_pa_s_kernel(
         identity = consts.tile([P, P], F32)
         make_identity(nc, identity[:])
 
-        minus_grid = consts.tile([P, GRID], F32)
-        nc.vector.tensor_scalar_mul(out=minus_grid[:], in0=grid_bf[:], scalar1=-1.0)
         minus_twice_grid = consts.tile([P, GRID], F32)
         nc.vector.tensor_scalar_mul(out=minus_twice_grid[:], in0=grid_bf[:], scalar1=-2.0)
+
+        def transpose_x(c):
+            x_t = psum_x.tile([P, HALVES, CHUNK_ROWS], F32)
+            for r in range(TILES_PER_CHUNK):
+                x_words = x_chunks[c][:, r, :].bitcast(F32)
+                for u in range(HALVES):
+                    nc.tensor.transpose(
+                        x_t[:, u, r * P : (r + 1) * P],
+                        x_words[:, u : FEATURES // PAIR : HALVES],
+                        identity[:],
+                    )
+            return x_t
+
+        x_transposed = [transpose_x(0)]
 
         spline_sorted = consts.tile([P, PACK, P], F32)
         nc.vector.tensor_copy(
@@ -93,40 +106,34 @@ def tile_advancedkanlayer_pa_s_kernel(
             in_=spline_grouped[:].rearrange("p u o t -> p (u o t)"),
         )
 
-        for c in range(CHUNKS):
-            x_sb = x_chunks[c]
-            x_t = psum_x.tile([P, HALVES, CHUNK_ROWS], F32)
-            for r in range(TILES_PER_CHUNK):
-                x_words = x_sb[:, r, :].bitcast(F32)
-                for u in range(HALVES):
-                    nc.tensor.transpose(
-                        x_t[:, u, r * P : (r + 1) * P],
-                        x_words[:, u : FEATURES // PAIR : HALVES],
-                        identity[:],
-                    )
+        for c in range(1, CHUNKS):
+            x_transposed.append(transpose_x(c))
+
+        def scalar_passes(c):
+            x_t = x_transposed[c]
             x_values = x_t[:].rearrange("p u n -> p (u n)").bitcast(BF16)
-
-            x_grouped = work.tile([P, CHUNK_ROWS, PACK], BF16, align_bytes=64)
-            nc.scalar.copy(out=x_grouped[:].bitcast(F32), in_=x_t[:].rearrange("p u n -> p n u"))
-
             twice_dist = work.tile([P, GRID, CHUNK_X], F32)
-            dist_sq = work.tile([P, GRID, CHUNK_X], F32)
-            gap_sq = work.tile([P, GRID, CHUNK_X], F32)
             for g in range(GRID):
                 nc.scalar.activation(
                     out=twice_dist[:, g, :], in_=x_values, func=ACT.Abs,
                     bias=minus_twice_grid[:, g : g + 1], scale=2.0,
                 )
-            for g in range(GRID):
-                nc.scalar.activation(
-                    out=dist_sq[:, g, :], in_=x_values, func=ACT.Square,
-                    bias=minus_grid[:, g : g + 1], scale=1.0,
-                )
-            nc.scalar.activation(out=gap_sq[:], in_=twice_dist[:], func=ACT.Square, bias=1.0, scale=-0.5)
-
             twice_gap = work.tile([P, GRID, CHUNK_X], F32)
+            nc.scalar.activation(
+                out=twice_gap[:, 0, :], in_=twice_dist[:, 0, :], func=ACT.Identity, bias=2.0, scale=-1.0
+            )
+            gap_sq = work.tile([P, GRID, CHUNK_X], F32)
+            nc.scalar.activation(out=gap_sq[:], in_=twice_dist[:], func=ACT.Square, bias=1.0, scale=-0.5)
+            dist_sq = work.tile([P, GRID, CHUNK_X], F32)
+            nc.scalar.activation(out=dist_sq[:], in_=twice_dist[:], func=ACT.Square, scale=0.5)
+            x_grouped = work.tile([P, CHUNK_ROWS, PACK], BF16, align_bytes=64)
+            nc.scalar.copy(out=x_grouped[:].bitcast(F32), in_=x_t[:].rearrange("p u n -> p n u"))
+            return twice_dist, twice_gap, gap_sq, dist_sq, x_grouped
+
+        def vector_pieces(twice_dist, twice_gap, gap_sq, dist_sq):
             nc.vector.tensor_scalar(
-                out=twice_gap[:], in0=twice_dist[:], scalar1=-1.0, scalar2=2.0, op0=ALU.mult, op1=ALU.add
+                out=twice_gap[:, 1, :], in0=twice_dist[:, 1, :], scalar1=-1.0, scalar2=2.0,
+                op0=ALU.mult, op1=ALU.add,
             )
             outer = work.tile([P, GRID, CHUNK_X], F32)
             nc.vector.scalar_tensor_tensor(
@@ -146,14 +153,9 @@ def tile_advancedkanlayer_pa_s_kernel(
                 op0=ALU.add,
                 op1=ALU.min,
             )
+            return basis
 
-            basis_codes = work.tile([P, HALVES, TILES_PER_CHUNK, P], U32, align_bytes=64)
-            basis_scales = work.tile([P, HALVES, TILES_PER_CHUNK, P], U8, align_bytes=64)
-            nc.vector.quantize_mx(
-                out=basis_codes[:].rearrange("p u r b -> p (u r b)").bitcast(FP8X4),
-                scales=basis_scales[:].rearrange("p u r b -> p (u r b)"),
-                in_=basis[:].rearrange("p n g -> p (n g)"),
-            )
+        def quantise_x(x_grouped):
             x_codes = work.tile([P, TILES_PER_CHUNK, P], U32, align_bytes=64)
             x_scales = work.tile([P, TILES_PER_CHUNK, P], U8, align_bytes=64)
             nc.vector.quantize_mx(
@@ -161,9 +163,30 @@ def tile_advancedkanlayer_pa_s_kernel(
                 scales=x_scales[:].rearrange("p r b -> p (r b)"),
                 in_=x_grouped[:].rearrange("p n t -> p (n t)"),
             )
+            return x_codes, x_scales
 
+        def quantise_basis(basis):
+            basis_codes = work.tile([P, HALVES, TILES_PER_CHUNK, P], U32, align_bytes=64)
+            basis_scales = work.tile([P, HALVES, TILES_PER_CHUNK, P], U8, align_bytes=64)
+            nc.vector.quantize_mx(
+                out=basis_codes[:].rearrange("p u r b -> p (u r b)").bitcast(FP8X4),
+                scales=basis_scales[:].rearrange("p u r b -> p (u r b)"),
+                in_=basis[:].rearrange("p n g -> p (n g)"),
+            )
+            return basis_codes, basis_scales
+
+        def multiply(x_codes, x_scales, basis_codes, basis_scales):
             sums = psum_out.tile([P, TILES_PER_CHUNK, 2, OUTPUTS], F32)
             for r in range(TILES_PER_CHUNK):
+                nc.tensor.matmul_mx(
+                    out=sums[:, r, 1, :],
+                    lhsT=x_codes[:, r, :].bitcast(FP8X4),
+                    lhsT_scale=x_scales[:, r, :],
+                    rhs=base_words[:].bitcast(FP4X4),
+                    rhs_scale=base_scales[:],
+                    start=True,
+                    stop=True,
+                )
                 for u in range(HALVES):
                     nc.tensor.matmul_mx(
                         out=sums[:, r, 0, :],
@@ -174,20 +197,30 @@ def tile_advancedkanlayer_pa_s_kernel(
                         start=(u == 0),
                         stop=(u == HALVES - 1),
                     )
-                nc.tensor.matmul_mx(
-                    out=sums[:, r, 1, :],
-                    lhsT=x_codes[:, r, :].bitcast(FP8X4),
-                    lhsT_scale=x_scales[:, r, :],
-                    rhs=base_words[:].bitcast(FP4X4),
-                    rhs_scale=base_scales[:],
-                    start=True,
-                    stop=True,
-                )
+            return sums
 
+        def scale_base(sums):
             tenth_base = work.tile([P, TILES_PER_CHUNK, OUTPUTS], F32)
             nc.scalar.mul(out=tenth_base[:], in_=sums[:, :, 1, :], mul=0.1)
+            return tenth_base
+
+        def add_and_store(c, sums, tenth_base):
             result = work.tile([P, TILES_PER_CHUNK, OUTPUTS], F32)
             nc.vector.tensor_add(out=result[:], in0=sums[:, :, 0, :], in1=tenth_base[:])
             nc.sync.dma_start(
                 out=out_rows[:, c * TILES_PER_CHUNK : (c + 1) * TILES_PER_CHUNK, :], in_=result[:]
             )
+
+        sums = None
+        for c in range(CHUNKS):
+            twice_dist, twice_gap, gap_sq, dist_sq, x_grouped = scalar_passes(c)
+            if c > 0:
+                tenth_base = scale_base(sums)
+            basis = vector_pieces(twice_dist, twice_gap, gap_sq, dist_sq)
+            x_codes, x_scales = quantise_x(x_grouped)
+            if c > 0:
+                add_and_store(c - 1, sums, tenth_base)
+            basis_codes, basis_scales = quantise_basis(basis)
+            sums = multiply(x_codes, x_scales, basis_codes, basis_scales)
+        tenth_base = scale_base(sums)
+        add_and_store(CHUNKS - 1, sums, tenth_base)

@@ -17,12 +17,12 @@ P = 128
 PACK = 4
 BATCH, FEATURES, OUTPUTS, GRID = 1280, 512, 128, 2
 ROW_TILES = BATCH // P
-TILES_PER_CHUNK = 2
-CHUNKS = ROW_TILES // TILES_PER_CHUNK
-CHUNK_ROWS = TILES_PER_CHUNK * P
+TILES_PER_BANK = 2
+BANKS = ROW_TILES // TILES_PER_BANK
+BANK_ROWS = TILES_PER_BANK * P
 HALVES = 2
 PAIR = 2
-CHUNK_X = HALVES * CHUNK_ROWS * PAIR
+BANK_X = HALVES * BANK_ROWS * PAIR
 
 FLOPS = 2 * BATCH * OUTPUTS * (FEATURES * GRID + FEATURES)
 
@@ -36,11 +36,11 @@ def tile_advancedkanlayer_pa_s_kernel(
 
     with ExitStack() as stack:
         consts = stack.enter_context(tc.tile_pool(name="consts", bufs=1))
-        loads = stack.enter_context(tc.tile_pool(name="loads", bufs=CHUNKS))
+        loads = stack.enter_context(tc.tile_pool(name="loads", bufs=BANKS))
         work = stack.enter_context(tc.tile_pool(name="work", bufs=3))
         psum_w = stack.enter_context(tc.psum_pool(name="psum_w", bufs=1))
-        psum_x = stack.enter_context(tc.psum_pool(name="psum_x", bufs=CHUNKS))
-        psum_out = stack.enter_context(tc.psum_pool(name="psum_out", bufs=2))
+        psum_x = stack.enter_context(tc.psum_pool(name="psum_x", bufs=BANKS))
+        psum_out = stack.enter_context(tc.psum_pool(name="psum_out", bufs=1))
         stack.enter_context(tc.manual_schedule())
 
         grid_bf = consts.tile([P, GRID], BF16)
@@ -48,13 +48,13 @@ def tile_advancedkanlayer_pa_s_kernel(
         spline_sb = consts.tile([P, FEATURES * GRID], BF16)
         nc.scalar.dma_start(out=spline_sb[:], in_=spline_weight.rearrange("o i g -> o (i g)"))
 
-        x_chunks = []
-        for c in range(CHUNKS):
-            x_sb = loads.tile([P, TILES_PER_CHUNK, FEATURES], BF16)
+        x_loaded = []
+        for bank in range(BANKS):
+            x_sb = loads.tile([P, TILES_PER_BANK, FEATURES], BF16)
             nc.sync.dma_start(
-                out=x_sb[:], in_=x_rows[:, c * TILES_PER_CHUNK : (c + 1) * TILES_PER_CHUNK, :]
+                out=x_sb[:], in_=x_rows[:, bank * TILES_PER_BANK : (bank + 1) * TILES_PER_BANK, :]
             )
-            x_chunks.append(x_sb)
+            x_loaded.append(x_sb)
 
         base_words = consts.tile([P, 2 * OUTPUTS], U8, align_bytes=64)
         base_scales = consts.tile([P, OUTPUTS], U8, align_bytes=64)
@@ -72,10 +72,10 @@ def tile_advancedkanlayer_pa_s_kernel(
         minus_twice_grid = consts.tile([P, GRID], F32)
         nc.vector.tensor_scalar_mul(out=minus_twice_grid[:], in0=grid_bf[:], scalar1=-2.0)
 
-        def transpose_x(c):
-            x_t = psum_x.tile([P, HALVES, CHUNK_ROWS], F32)
-            for r in range(TILES_PER_CHUNK):
-                x_words = x_chunks[c][:, r, :].bitcast(F32)
+        def transpose_x(bank):
+            x_t = psum_x.tile([P, HALVES, BANK_ROWS], F32)
+            for r in range(TILES_PER_BANK):
+                x_words = x_loaded[bank][:, r, :].bitcast(F32)
                 for u in range(HALVES):
                     nc.tensor.transpose(
                         x_t[:, u, r * P : (r + 1) * P],
@@ -106,45 +106,53 @@ def tile_advancedkanlayer_pa_s_kernel(
             in_=spline_grouped[:].rearrange("p u o t -> p (u o t)"),
         )
 
-        for c in range(1, CHUNKS):
-            x_transposed.append(transpose_x(c))
+        for bank in range(1, BANKS):
+            x_transposed.append(transpose_x(bank))
 
-        def scalar_passes(c):
-            x_t = x_transposed[c]
+        def scalar_passes(bank, scalar_planes):
+            x_t = x_transposed[bank]
             x_values = x_t[:].rearrange("p u n -> p (u n)").bitcast(BF16)
-            twice_dist = work.tile([P, GRID, CHUNK_X], F32)
+            twice_dist = work.tile([P, GRID, BANK_X], F32)
             for g in range(GRID):
                 nc.scalar.activation(
                     out=twice_dist[:, g, :], in_=x_values, func=ACT.Abs,
                     bias=minus_twice_grid[:, g : g + 1], scale=2.0,
                 )
-            twice_gap = work.tile([P, GRID, CHUNK_X], F32)
-            nc.scalar.activation(
-                out=twice_gap[:, 0, :], in_=twice_dist[:, 0, :], func=ACT.Identity, bias=2.0, scale=-1.0
-            )
-            gap_sq = work.tile([P, GRID, CHUNK_X], F32)
-            nc.scalar.activation(out=gap_sq[:], in_=twice_dist[:], func=ACT.Square, bias=1.0, scale=-0.5)
-            dist_sq = work.tile([P, GRID, CHUNK_X], F32)
-            nc.scalar.activation(out=dist_sq[:], in_=twice_dist[:], func=ACT.Square, scale=0.5)
-            x_grouped = work.tile([P, CHUNK_ROWS, PACK], BF16, align_bytes=64)
+            x_grouped = work.tile([P, BANK_ROWS, PACK], BF16, align_bytes=64)
             nc.scalar.copy(out=x_grouped[:].bitcast(F32), in_=x_t[:].rearrange("p u n -> p n u"))
+            twice_gap = work.tile([P, GRID, BANK_X], F32)
+            if scalar_planes > 0:
+                nc.scalar.activation(
+                    out=twice_gap[:, :scalar_planes, :], in_=twice_dist[:, :scalar_planes, :],
+                    func=ACT.Identity, bias=2.0, scale=-1.0,
+                )
+            gap_sq = work.tile([P, GRID, BANK_X], F32)
+            nc.scalar.activation(out=gap_sq[:], in_=twice_dist[:], func=ACT.Square, bias=1.0, scale=-0.5)
+            dist_sq = work.tile([P, GRID, BANK_X], F32)
+            nc.scalar.activation(out=dist_sq[:], in_=twice_dist[:], func=ACT.Square, scale=0.5)
             return twice_dist, twice_gap, gap_sq, dist_sq, x_grouped
 
-        def vector_pieces(twice_dist, twice_gap, gap_sq, dist_sq):
-            nc.vector.tensor_scalar(
-                out=twice_gap[:, 1, :], in0=twice_dist[:, 1, :], scalar1=-1.0, scalar2=2.0,
-                op0=ALU.mult, op1=ALU.add,
-            )
-            outer = work.tile([P, GRID, CHUNK_X], F32)
+        def other_planes_of_twice_gap(scalar_planes, twice_dist, twice_gap):
+            if scalar_planes < GRID:
+                nc.vector.tensor_scalar(
+                    out=twice_gap[:, scalar_planes:, :], in0=twice_dist[:, scalar_planes:, :],
+                    scalar1=-1.0, scalar2=2.0, op0=ALU.mult, op1=ALU.add,
+                )
+
+        def outer_piece(twice_gap, gap_sq):
             nc.vector.scalar_tensor_tensor(
-                out=outer[:], in0=twice_gap[:], scalar=0.0, in1=gap_sq[:], op0=ALU.max, op1=ALU.mult
+                out=gap_sq[:], in0=twice_gap[:], scalar=0.0, in1=gap_sq[:], op0=ALU.max, op1=ALU.mult
             )
-            inner_less_one = work.tile([P, GRID, CHUNK_X], F32)
+            return gap_sq
+
+        def inner_piece_less_one(twice_gap, dist_sq):
             nc.vector.scalar_tensor_tensor(
-                out=inner_less_one[:], in0=dist_sq[:], scalar=-3.0, in1=twice_gap[:],
-                op0=ALU.mult, op1=ALU.mult,
+                out=dist_sq[:], in0=dist_sq[:], scalar=-3.0, in1=twice_gap[:], op0=ALU.mult, op1=ALU.mult
             )
-            basis = work.tile([P, CHUNK_X, GRID], BF16, align_bytes=64)
+            return dist_sq
+
+        def smaller_piece(outer, inner_less_one):
+            basis = work.tile([P, BANK_X, GRID], BF16, align_bytes=64)
             nc.vector.scalar_tensor_tensor(
                 out=basis[:],
                 in0=inner_less_one[:].rearrange("p g n -> p n g"),
@@ -155,31 +163,18 @@ def tile_advancedkanlayer_pa_s_kernel(
             )
             return basis
 
-        def quantise_x(x_grouped):
-            x_codes = work.tile([P, TILES_PER_CHUNK, P], U32, align_bytes=64)
-            x_scales = work.tile([P, TILES_PER_CHUNK, P], U8, align_bytes=64)
+        def base_product(x_grouped):
+            x_codes = work.tile([P, TILES_PER_BANK, P], U32, align_bytes=64)
+            x_scales = work.tile([P, TILES_PER_BANK, P], U8, align_bytes=64)
             nc.vector.quantize_mx(
                 out=x_codes[:].rearrange("p r b -> p (r b)").bitcast(FP8X4),
                 scales=x_scales[:].rearrange("p r b -> p (r b)"),
                 in_=x_grouped[:].rearrange("p n t -> p (n t)"),
             )
-            return x_codes, x_scales
-
-        def quantise_basis(basis):
-            basis_codes = work.tile([P, HALVES, TILES_PER_CHUNK, P], U32, align_bytes=64)
-            basis_scales = work.tile([P, HALVES, TILES_PER_CHUNK, P], U8, align_bytes=64)
-            nc.vector.quantize_mx(
-                out=basis_codes[:].rearrange("p u r b -> p (u r b)").bitcast(FP8X4),
-                scales=basis_scales[:].rearrange("p u r b -> p (u r b)"),
-                in_=basis[:].rearrange("p n g -> p (n g)"),
-            )
-            return basis_codes, basis_scales
-
-        def multiply(x_codes, x_scales, basis_codes, basis_scales):
-            sums = psum_out.tile([P, TILES_PER_CHUNK, 2, OUTPUTS], F32)
-            for r in range(TILES_PER_CHUNK):
+            base_sums = psum_out.tile([P, TILES_PER_BANK, OUTPUTS], F32)
+            for r in range(TILES_PER_BANK):
                 nc.tensor.matmul_mx(
-                    out=sums[:, r, 1, :],
+                    out=base_sums[:, r, :],
                     lhsT=x_codes[:, r, :].bitcast(FP8X4),
                     lhsT_scale=x_scales[:, r, :],
                     rhs=base_words[:].bitcast(FP4X4),
@@ -187,9 +182,26 @@ def tile_advancedkanlayer_pa_s_kernel(
                     start=True,
                     stop=True,
                 )
+            return base_sums
+
+        def a_tenth_of(base_sums):
+            tenth_base = work.tile([P, TILES_PER_BANK, OUTPUTS], F32)
+            nc.scalar.mul(out=tenth_base[:], in_=base_sums[:], mul=0.1)
+            return tenth_base
+
+        def spline_product(basis):
+            basis_codes = work.tile([P, HALVES, TILES_PER_BANK, P], U32, align_bytes=64)
+            basis_scales = work.tile([P, HALVES, TILES_PER_BANK, P], U8, align_bytes=64)
+            nc.vector.quantize_mx(
+                out=basis_codes[:].rearrange("p u r b -> p (u r b)").bitcast(FP8X4),
+                scales=basis_scales[:].rearrange("p u r b -> p (u r b)"),
+                in_=basis[:].rearrange("p n g -> p (n g)"),
+            )
+            spline_sums = psum_out.tile([P, TILES_PER_BANK, OUTPUTS], F32)
+            for r in range(TILES_PER_BANK):
                 for u in range(HALVES):
                     nc.tensor.matmul_mx(
-                        out=sums[:, r, 0, :],
+                        out=spline_sums[:, r, :],
                         lhsT=basis_codes[:, u, r, :].bitcast(FP8X4),
                         lhsT_scale=basis_scales[:, u, r, :],
                         rhs=spline_codes[:, u, :].bitcast(FP8X4),
@@ -197,30 +209,30 @@ def tile_advancedkanlayer_pa_s_kernel(
                         start=(u == 0),
                         stop=(u == HALVES - 1),
                     )
-            return sums
+            return spline_sums
 
-        def scale_base(sums):
-            tenth_base = work.tile([P, TILES_PER_CHUNK, OUTPUTS], F32)
-            nc.scalar.mul(out=tenth_base[:], in_=sums[:, :, 1, :], mul=0.1)
-            return tenth_base
-
-        def add_and_store(c, sums, tenth_base):
-            result = work.tile([P, TILES_PER_CHUNK, OUTPUTS], F32)
-            nc.vector.tensor_add(out=result[:], in0=sums[:, :, 0, :], in1=tenth_base[:])
+        def add_and_store(bank, spline_sums, tenth_base):
+            result = work.tile([P, TILES_PER_BANK, OUTPUTS], F32)
+            nc.vector.tensor_add(out=result[:], in0=spline_sums[:], in1=tenth_base[:])
             nc.sync.dma_start(
-                out=out_rows[:, c * TILES_PER_CHUNK : (c + 1) * TILES_PER_CHUNK, :], in_=result[:]
+                out=out_rows[:, bank * TILES_PER_BANK : (bank + 1) * TILES_PER_BANK, :], in_=result[:]
             )
 
-        sums = None
-        for c in range(CHUNKS):
-            twice_dist, twice_gap, gap_sq, dist_sq, x_grouped = scalar_passes(c)
-            if c > 0:
-                tenth_base = scale_base(sums)
-            basis = vector_pieces(twice_dist, twice_gap, gap_sq, dist_sq)
-            x_codes, x_scales = quantise_x(x_grouped)
-            if c > 0:
-                add_and_store(c - 1, sums, tenth_base)
-            basis_codes, basis_scales = quantise_basis(basis)
-            sums = multiply(x_codes, x_scales, basis_codes, basis_scales)
-        tenth_base = scale_base(sums)
-        add_and_store(CHUNKS - 1, sums, tenth_base)
+        basis, base_sums = None, None
+        for bank in range(BANKS):
+            scalar_planes = (1 if bank > 0 else 0) + (1 if bank == BANKS - 1 else 0)
+            twice_dist, twice_gap, gap_sq, dist_sq, x_grouped = scalar_passes(bank, scalar_planes)
+            if bank > 0:
+                tenth_base = a_tenth_of(base_sums)
+            other_planes_of_twice_gap(scalar_planes, twice_dist, twice_gap)
+            if bank > 0:
+                spline_sums = spline_product(basis)
+            base_sums = base_product(x_grouped)
+            outer = outer_piece(twice_gap, gap_sq)
+            if bank > 0:
+                add_and_store(bank - 1, spline_sums, tenth_base)
+            inner_less_one = inner_piece_less_one(twice_gap, dist_sq)
+            basis = smaller_piece(outer, inner_less_one)
+        tenth_base = a_tenth_of(base_sums)
+        spline_sums = spline_product(basis)
+        add_and_store(BANKS - 1, spline_sums, tenth_base)

@@ -22,15 +22,29 @@ BANKS = ROW_TILES // TILES_PER_BANK
 BANK_ROWS = TILES_PER_BANK * P
 HALVES = 2
 PAIR = 2
-BANK_X = HALVES * BANK_ROWS * PAIR
+BANK_TILES = 4
+
+CHUNKS = [(0, 0, 1), (0, 1, 1), (1, 0, 2), (2, 0, 2), (3, 0, 2), (4, 0, 1), (4, 1, 1)]
+SCALAR_ROOT_GAPS_FROM = 4
 
 FLOPS = 2 * BATCH * OUTPUTS * (FEATURES * GRID + FEATURES)
+
+
+def real_root_of_inner_piece():
+    root = -0.3
+    for step in range(60):
+        root = root - (6.0 * root**3 - 6.0 * root**2 + 1.0) / (18.0 * root**2 - 12.0 * root)
+    return root
 
 
 def tile_advancedkanlayer_pa_s_kernel(
     tc, x_norm, spline_weight, base_activation_words, base_activation_scales, grid_points, out
 ):
     nc = tc.nc
+    root = real_root_of_inner_piece()
+    beta = (root - 1.0) / 2.0
+    gamma = (root - 1.0) * (3.0 * root + 1.0) / 4.0
+
     x_rows = x_norm.rearrange("(p r) i -> p r i", r=ROW_TILES)
     out_rows = out.rearrange("(p r) o -> p r o", r=ROW_TILES)
 
@@ -38,7 +52,6 @@ def tile_advancedkanlayer_pa_s_kernel(
         consts = stack.enter_context(tc.tile_pool(name="consts", bufs=1))
         loads = stack.enter_context(tc.tile_pool(name="loads", bufs=BANKS))
         work = stack.enter_context(tc.tile_pool(name="work", bufs=3))
-        psum_w = stack.enter_context(tc.psum_pool(name="psum_w", bufs=1))
         psum_x = stack.enter_context(tc.psum_pool(name="psum_x", bufs=BANKS))
         psum_out = stack.enter_context(tc.psum_pool(name="psum_out", bufs=1))
         stack.enter_context(tc.manual_schedule())
@@ -73,7 +86,7 @@ def tile_advancedkanlayer_pa_s_kernel(
         nc.vector.tensor_scalar_mul(out=minus_twice_grid[:], in0=grid_bf[:], scalar1=-2.0)
 
         def transpose_x(bank):
-            x_t = psum_x.tile([P, HALVES, BANK_ROWS], F32)
+            x_t = psum_x.tile([P, HALVES, BANK_ROWS], F32, tag="x_t")
             for r in range(TILES_PER_BANK):
                 x_words = x_loaded[bank][:, r, :].bitcast(F32)
                 for u in range(HALVES):
@@ -84,95 +97,116 @@ def tile_advancedkanlayer_pa_s_kernel(
                     )
             return x_t
 
+        spline_t = psum_x.tile([P, PACK, OUTPUTS], F32, tag="x_t")
         x_transposed = [transpose_x(0)]
 
         spline_sorted = consts.tile([P, PACK, P], F32)
         nc.vector.tensor_copy(
             out=spline_sorted[:], in_=spline_sb[:].bitcast(F32).rearrange("o (p j) -> o j p", j=PACK)
         )
-        spline_t = psum_w.tile([P, PACK, OUTPUTS], F32)
         for j in range(PACK):
             nc.tensor.transpose(spline_t[:, j, :], spline_sorted[:, j, :], identity[:])
-        spline_grouped = consts.tile([P, HALVES, OUTPUTS, PACK], BF16, align_bytes=64)
+        spline_grouped = consts.tile([P, GRID, OUTPUTS, PACK], BF16, align_bytes=64)
         nc.vector.tensor_copy(
-            out=spline_grouped[:].bitcast(F32),
-            in_=spline_t[:].rearrange("p (u e) o -> p u o e", u=HALVES),
+            out=spline_grouped[:],
+            in_=spline_t[:]
+            .rearrange("p j o -> p (j o)")
+            .bitcast(BF16)
+            .rearrange("p (j o g) -> p g o j", j=PACK, g=GRID),
         )
-        spline_codes = consts.tile([P, HALVES, OUTPUTS], U32, align_bytes=64)
-        spline_scales = consts.tile([P, HALVES, OUTPUTS], U8, align_bytes=64)
+        spline_codes = consts.tile([P, GRID, OUTPUTS], U32, align_bytes=64)
+        spline_scales = consts.tile([P, GRID, OUTPUTS], U8, align_bytes=64)
         nc.vector.quantize_mx(
-            out=spline_codes[:].rearrange("p u o -> p (u o)").bitcast(FP8X4),
-            scales=spline_scales[:].rearrange("p u o -> p (u o)"),
-            in_=spline_grouped[:].rearrange("p u o t -> p (u o t)"),
+            out=spline_codes[:].rearrange("p g o -> p (g o)").bitcast(FP8X4),
+            scales=spline_scales[:].rearrange("p g o -> p (g o)"),
+            in_=spline_grouped[:].rearrange("p g o t -> p (g o t)"),
         )
 
         for bank in range(1, BANKS):
             x_transposed.append(transpose_x(bank))
 
-        def scalar_passes(bank, scalar_planes):
-            x_t = x_transposed[bank]
-            x_values = x_t[:].rearrange("p u n -> p (u n)").bitcast(BF16)
-            twice_dist = work.tile([P, GRID, BANK_X], F32)
+        def twice_distance(bank, first, tiles):
+            rows = tiles * P
+            x_values = (
+                x_transposed[bank][:]
+                .rearrange("p u n -> p (u n)")
+                .bitcast(BF16)
+                .rearrange("p (u n e) -> p n u e", u=HALVES, e=PAIR)[:, first * P : first * P + rows, :, :]
+            )
+            twice_dist = work.tile([P, GRID, rows * PACK], F32)
             for g in range(GRID):
                 nc.scalar.activation(
-                    out=twice_dist[:, g, :], in_=x_values, func=ACT.Abs,
-                    bias=minus_twice_grid[:, g : g + 1], scale=2.0,
+                    out=twice_dist[:, g, :].rearrange("p (n u e) -> p n u e", u=HALVES, e=PAIR),
+                    in_=x_values, func=ACT.Abs, bias=minus_twice_grid[:, g : g + 1], scale=2.0,
                 )
-            x_grouped = work.tile([P, BANK_ROWS, PACK], BF16, align_bytes=64)
-            nc.scalar.copy(out=x_grouped[:].bitcast(F32), in_=x_t[:].rearrange("p u n -> p n u"))
-            twice_gap = work.tile([P, GRID, BANK_X], F32)
-            if scalar_planes > 0:
-                nc.scalar.activation(
-                    out=twice_gap[:, :scalar_planes, :], in_=twice_dist[:, :scalar_planes, :],
-                    func=ACT.Identity, bias=2.0, scale=-1.0,
-                )
-            gap_sq = work.tile([P, GRID, BANK_X], F32)
-            nc.scalar.activation(out=gap_sq[:], in_=twice_dist[:], func=ACT.Square, bias=1.0, scale=-0.5)
-            dist_sq = work.tile([P, GRID, BANK_X], F32)
-            nc.scalar.activation(out=dist_sq[:], in_=twice_dist[:], func=ACT.Square, scale=0.5)
-            return twice_dist, twice_gap, gap_sq, dist_sq, x_grouped
+            return twice_dist
 
-        def other_planes_of_twice_gap(scalar_planes, twice_dist, twice_gap):
-            if scalar_planes < GRID:
-                nc.vector.tensor_scalar(
-                    out=twice_gap[:, scalar_planes:, :], in0=twice_dist[:, scalar_planes:, :],
-                    scalar1=-1.0, scalar2=2.0, op0=ALU.mult, op1=ALU.add,
-                )
-
-        def outer_piece(twice_gap, gap_sq):
-            nc.vector.scalar_tensor_tensor(
-                out=gap_sq[:], in0=twice_gap[:], scalar=0.0, in1=gap_sq[:], op0=ALU.max, op1=ALU.mult
+        def regroup_x(bank, first, tiles):
+            rows = tiles * P
+            x_grouped = work.tile([P, rows, PACK], BF16, align_bytes=64)
+            nc.scalar.copy(
+                out=x_grouped[:].bitcast(F32),
+                in_=x_transposed[bank][:, :, first * P : first * P + rows].rearrange("p u n -> p n u"),
             )
+            return x_grouped
+
+        def gap_squared(twice_dist, tiles):
+            gap_sq = work.tile([P, GRID, tiles * P * PACK], F32)
+            nc.scalar.activation(out=gap_sq[:], in_=twice_dist[:], func=ACT.Square, bias=1.0, scale=-0.5)
             return gap_sq
 
-        def inner_piece_less_one(twice_gap, dist_sq):
-            nc.vector.scalar_tensor_tensor(
-                out=dist_sq[:], in0=dist_sq[:], scalar=-3.0, in1=twice_gap[:], op0=ALU.mult, op1=ALU.mult
-            )
-            return dist_sq
+        def shifted_squared(twice_dist, tiles):
+            shifted_sq = work.tile([P, GRID, tiles * P * PACK], F32)
+            nc.scalar.activation(out=shifted_sq[:], in_=twice_dist[:], func=ACT.Square, bias=beta, scale=0.5)
+            return shifted_sq
 
-        def smaller_piece(outer, inner_less_one):
-            basis = work.tile([P, BANK_X, GRID], BF16, align_bytes=64)
-            nc.vector.scalar_tensor_tensor(
-                out=basis[:],
-                in0=inner_less_one[:].rearrange("p g n -> p n g"),
-                scalar=1.0,
-                in1=outer[:].rearrange("p g n -> p n g"),
-                op0=ALU.add,
-                op1=ALU.min,
-            )
-            return basis
+        def six_root_gaps(twice_dist, tiles, on_scalar):
+            root_gap = work.tile([P, GRID, tiles * P * PACK], F32)
+            if on_scalar:
+                nc.scalar.activation(
+                    out=root_gap[:], in_=twice_dist[:], func=ACT.Identity, bias=6.0 * root, scale=-3.0
+                )
+            else:
+                nc.vector.tensor_scalar(
+                    out=root_gap[:], in0=twice_dist[:], scalar1=-3.0, scalar2=6.0 * root,
+                    op0=ALU.mult, op1=ALU.add,
+                )
+            return root_gap
 
-        def base_product(x_grouped):
-            x_codes = work.tile([P, TILES_PER_BANK, P], U32, align_bytes=64)
-            x_scales = work.tile([P, TILES_PER_BANK, P], U8, align_bytes=64)
+        def minus_outer_piece(twice_dist, gap_sq, tiles):
+            minus_outer = work.tile([P, GRID, tiles * P * PACK], BF16)
+            nc.vector.scalar_tensor_tensor(
+                out=minus_outer[:], in0=twice_dist[:], scalar=2.0, in1=gap_sq[:],
+                op0=ALU.subtract, op1=ALU.mult,
+            )
+            return minus_outer
+
+        def minus_inner_piece(shifted_sq, root_gap, tiles):
+            minus_inner = work.tile([P, GRID, tiles * P * PACK], BF16)
+            nc.vector.scalar_tensor_tensor(
+                out=minus_inner[:], in0=shifted_sq[:], scalar=gamma, in1=root_gap[:],
+                op0=ALU.add, op1=ALU.mult,
+            )
+            return minus_inner
+
+        def larger_piece(minus_outer, minus_inner, tiles):
+            minus_basis = work.tile([P, GRID, tiles * P * PACK], BF16, align_bytes=64)
+            nc.vector.tensor_tensor(out=minus_basis[:], in0=minus_outer[:], in1=minus_inner[:], op=ALU.max)
+            return minus_basis
+
+        def clamp_at_zero(minus_basis):
+            nc.vector.tensor_scalar_min(out=minus_basis[:], in0=minus_basis[:], scalar1=0.0)
+
+        def base_product(x_grouped, tiles):
+            x_codes = work.tile([P, tiles, P], U32, align_bytes=64)
+            x_scales = work.tile([P, tiles, P], U8, align_bytes=64)
             nc.vector.quantize_mx(
                 out=x_codes[:].rearrange("p r b -> p (r b)").bitcast(FP8X4),
                 scales=x_scales[:].rearrange("p r b -> p (r b)"),
                 in_=x_grouped[:].rearrange("p n t -> p (n t)"),
             )
-            base_sums = psum_out.tile([P, TILES_PER_BANK, OUTPUTS], F32)
-            for r in range(TILES_PER_BANK):
+            base_sums = psum_out.tile([P, BANK_TILES, OUTPUTS], F32, bufs=2)
+            for r in range(tiles):
                 nc.tensor.matmul_mx(
                     out=base_sums[:, r, :],
                     lhsT=x_codes[:, r, :].bitcast(FP8X4),
@@ -184,55 +218,68 @@ def tile_advancedkanlayer_pa_s_kernel(
                 )
             return base_sums
 
-        def a_tenth_of(base_sums):
-            tenth_base = work.tile([P, TILES_PER_BANK, OUTPUTS], F32)
-            nc.scalar.mul(out=tenth_base[:], in_=base_sums[:], mul=0.1)
+        def a_tenth_of(base_sums, tiles):
+            tenth_base = work.tile([P, tiles, OUTPUTS], F32)
+            nc.scalar.mul(out=tenth_base[:], in_=base_sums[:, :tiles, :], mul=0.1)
             return tenth_base
 
-        def spline_product(basis):
-            basis_codes = work.tile([P, HALVES, TILES_PER_BANK, P], U32, align_bytes=64)
-            basis_scales = work.tile([P, HALVES, TILES_PER_BANK, P], U8, align_bytes=64)
+        def minus_spline_product(minus_basis, tiles):
+            basis_codes = work.tile([P, GRID, tiles, P], U32, align_bytes=64)
+            basis_scales = work.tile([P, GRID, tiles, P], U8, align_bytes=64)
             nc.vector.quantize_mx(
-                out=basis_codes[:].rearrange("p u r b -> p (u r b)").bitcast(FP8X4),
-                scales=basis_scales[:].rearrange("p u r b -> p (u r b)"),
-                in_=basis[:].rearrange("p n g -> p (n g)"),
+                out=basis_codes[:].rearrange("p g r b -> p (g r b)").bitcast(FP8X4),
+                scales=basis_scales[:].rearrange("p g r b -> p (g r b)"),
+                in_=minus_basis[:].rearrange("p g n -> p (g n)"),
             )
-            spline_sums = psum_out.tile([P, TILES_PER_BANK, OUTPUTS], F32)
-            for r in range(TILES_PER_BANK):
-                for u in range(HALVES):
+            minus_spline = psum_out.tile([P, BANK_TILES, OUTPUTS], F32)
+            for r in range(tiles):
+                for g in range(GRID):
                     nc.tensor.matmul_mx(
-                        out=spline_sums[:, r, :],
-                        lhsT=basis_codes[:, u, r, :].bitcast(FP8X4),
-                        lhsT_scale=basis_scales[:, u, r, :],
-                        rhs=spline_codes[:, u, :].bitcast(FP8X4),
-                        rhs_scale=spline_scales[:, u, :],
-                        start=(u == 0),
-                        stop=(u == HALVES - 1),
+                        out=minus_spline[:, r, :],
+                        lhsT=basis_codes[:, g, r, :].bitcast(FP8X4),
+                        lhsT_scale=basis_scales[:, g, r, :],
+                        rhs=spline_codes[:, g, :].bitcast(FP8X4),
+                        rhs_scale=spline_scales[:, g, :],
+                        start=(g == 0),
+                        stop=(g == GRID - 1),
                     )
-            return spline_sums
+            return minus_spline
 
-        def add_and_store(bank, spline_sums, tenth_base):
-            result = work.tile([P, TILES_PER_BANK, OUTPUTS], F32)
-            nc.vector.tensor_add(out=result[:], in0=spline_sums[:], in1=tenth_base[:])
-            nc.sync.dma_start(
-                out=out_rows[:, bank * TILES_PER_BANK : (bank + 1) * TILES_PER_BANK, :], in_=result[:]
-            )
+        def subtract_and_store(bank, first, tiles, tenth_base, minus_spline):
+            result = work.tile([P, tiles, OUTPUTS], F32)
+            nc.vector.tensor_sub(out=result[:], in0=tenth_base[:], in1=minus_spline[:, :tiles, :])
+            tile0 = bank * TILES_PER_BANK + first
+            nc.sync.dma_start(out=out_rows[:, tile0 : tile0 + tiles, :], in_=result[:])
 
-        basis, base_sums = None, None
-        for bank in range(BANKS):
-            scalar_planes = (1 if bank > 0 else 0) + (1 if bank == BANKS - 1 else 0)
-            twice_dist, twice_gap, gap_sq, dist_sq, x_grouped = scalar_passes(bank, scalar_planes)
-            if bank > 0:
-                tenth_base = a_tenth_of(base_sums)
-            other_planes_of_twice_gap(scalar_planes, twice_dist, twice_gap)
-            if bank > 0:
-                spline_sums = spline_product(basis)
-            base_sums = base_product(x_grouped)
-            outer = outer_piece(twice_gap, gap_sq)
-            if bank > 0:
-                add_and_store(bank - 1, spline_sums, tenth_base)
-            inner_less_one = inner_piece_less_one(twice_gap, dist_sq)
-            basis = smaller_piece(outer, inner_less_one)
-        tenth_base = a_tenth_of(base_sums)
-        spline_sums = spline_product(basis)
-        add_and_store(BANKS - 1, spline_sums, tenth_base)
+        chunks = CHUNKS
+        last = len(chunks) - 1
+        minus_outer, minus_inner, minus_basis = {}, {}, {}
+        base_sums, tenth_base, minus_spline = {}, {}, {}
+        for c in range(len(chunks) + 2):
+            if c >= 2:
+                tenth_base[c - 2] = a_tenth_of(base_sums[c - 2], chunks[c - 2][2])
+            if c <= last:
+                bank, first, tiles = chunks[c]
+                on_scalar = c >= SCALAR_ROOT_GAPS_FROM
+                twice_dist = twice_distance(bank, first, tiles)
+                x_grouped = regroup_x(bank, first, tiles)
+                gap_sq = gap_squared(twice_dist, tiles)
+                if on_scalar:
+                    root_gap = six_root_gaps(twice_dist, tiles, True)
+                shifted_sq = shifted_squared(twice_dist, tiles)
+            if c <= last:
+                base_sums[c] = base_product(x_grouped, tiles)
+                if not on_scalar:
+                    root_gap = six_root_gaps(twice_dist, tiles, False)
+            if 1 <= c <= last + 1:
+                minus_basis[c - 1] = larger_piece(minus_outer[c - 1], minus_inner[c - 1], chunks[c - 1][2])
+            if c <= last:
+                minus_outer[c] = minus_outer_piece(twice_dist, gap_sq, tiles)
+            if 1 <= c <= last + 1:
+                clamp_at_zero(minus_basis[c - 1])
+            if c >= 2:
+                subtract_and_store(chunks[c - 2][0], chunks[c - 2][1], chunks[c - 2][2], tenth_base[c - 2], minus_spline[c - 2])
+            if c <= last:
+                minus_inner[c] = minus_inner_piece(shifted_sq, root_gap, tiles)
+            if 1 <= c <= last + 1:
+                minus_spline[c - 1] = minus_spline_product(minus_basis[c - 1], chunks[c - 1][2])

@@ -17,15 +17,21 @@ P = 128
 PACK = 4
 BATCH, FEATURES, OUTPUTS, GRID = 1280, 512, 128, 2
 ROW_TILES = BATCH // P
+UNITS = ROW_TILES * GRID
+QUARTER = FEATURES // PACK
+BLOCK_ROWS = P // PACK
+BLOCKS = P // BLOCK_ROWS
+TILE_X = P * PACK
 TILES_PER_BANK = 2
 BANKS = ROW_TILES // TILES_PER_BANK
 BANK_ROWS = TILES_PER_BANK * P
 HALVES = 2
 PAIR = 2
-BANK_TILES = 4
-
-CHUNKS = [(0, 0, 1), (0, 1, 1), (1, 0, 2), (2, 0, 2), (3, 0, 2), (4, 0, 1), (4, 1, 1)]
-SCALAR_ROOT_GAPS_FROM = 4
+GROUP_TILES = 4
+BANKS_PER_GROUP = GROUP_TILES // TILES_PER_BANK
+AHEAD = 3
+QUANTISE_X_AT = [2, 4, 6]
+TENTH_AT = [4, 6, 8]
 
 FLOPS = 2 * BATCH * OUTPUTS * (FEATURES * GRID + FEATURES)
 
@@ -44,15 +50,18 @@ def tile_advancedkanlayer_pa_s_kernel(
     root = real_root_of_inner_piece()
     beta = (root - 1.0) / 2.0
     gamma = (root - 1.0) * (3.0 * root + 1.0) / 4.0
+    sqrt3 = 3.0**0.5
 
-    x_rows = x_norm.rearrange("(p r) i -> p r i", r=ROW_TILES)
-    out_rows = out.rearrange("(p r) o -> p r o", r=ROW_TILES)
+    x_quarters = x_norm.rearrange("(m n) (j q) -> (n j) m q", n=BLOCK_ROWS, j=PACK)
+    x_rows = x_norm.rearrange("(r p) i -> p r i", p=P)
+    out_rows = out.rearrange("(r p) o -> p r o", p=P)
 
     with ExitStack() as stack:
         consts = stack.enter_context(tc.tile_pool(name="consts", bufs=1))
         loads = stack.enter_context(tc.tile_pool(name="loads", bufs=BANKS))
         work = stack.enter_context(tc.tile_pool(name="work", bufs=3))
-        psum_x = stack.enter_context(tc.psum_pool(name="psum_x", bufs=BANKS))
+        psum_s = stack.enter_context(tc.psum_pool(name="psum_s", bufs=5))
+        psum_x = stack.enter_context(tc.psum_pool(name="psum_x", bufs=1))
         psum_out = stack.enter_context(tc.psum_pool(name="psum_out", bufs=1))
         stack.enter_context(tc.manual_schedule())
 
@@ -61,141 +70,145 @@ def tile_advancedkanlayer_pa_s_kernel(
         spline_sb = consts.tile([P, FEATURES * GRID], BF16)
         nc.scalar.dma_start(out=spline_sb[:], in_=spline_weight.rearrange("o i g -> o (i g)"))
 
-        x_loaded = []
-        for bank in range(BANKS):
-            x_sb = loads.tile([P, TILES_PER_BANK, FEATURES], BF16)
-            nc.sync.dma_start(
-                out=x_sb[:], in_=x_rows[:, bank * TILES_PER_BANK : (bank + 1) * TILES_PER_BANK, :]
-            )
-            x_loaded.append(x_sb)
-
         base_words = consts.tile([P, 2 * OUTPUTS], U8, align_bytes=64)
         base_scales = consts.tile([P, OUTPUTS], U8, align_bytes=64)
         nc.vector.memset(base_scales[:].bitcast(I32), 0)
-        nc.sync.dma_start(out=base_words[:].bitcast(I32), in_=base_activation_words[0].bitcast(I32))
-        for quadrant in range(4):
-            nc.sync.dma_start(
-                out=base_scales[32 * quadrant : 32 * quadrant + 4, :].bitcast(I32),
-                in_=base_activation_scales[0, 4 * quadrant : 4 * quadrant + 4, :].bitcast(I32),
-            )
+
+        quarters_loaded, rows_loaded = [], []
+        for bank in range(BANKS):
+            xq_sb = loads.tile([P, TILES_PER_BANK * BLOCKS, QUARTER], BF16)
+            pieces = TILES_PER_BANK if bank == 0 else 1
+            width = TILES_PER_BANK * BLOCKS // pieces
+            for m in range(0, TILES_PER_BANK * BLOCKS, width):
+                block0 = bank * TILES_PER_BANK * BLOCKS + m
+                nc.sync.dma_start(out=xq_sb[:, m : m + width, :], in_=x_quarters[:, block0 : block0 + width, :])
+            quarters_loaded.append(xq_sb)
+            if bank > 0:
+                xr_sb = loads.tile([P, TILES_PER_BANK, FEATURES], BF16)
+                tile0 = (bank - 1) * TILES_PER_BANK
+                nc.sync.dma_start(out=xr_sb[:], in_=x_rows[:, tile0 : tile0 + TILES_PER_BANK, :])
+                rows_loaded.append(xr_sb)
+            if bank == 1:
+                nc.sync.dma_start(out=base_words[:].bitcast(I32), in_=base_activation_words[0].bitcast(I32))
+                for quadrant in range(4):
+                    nc.sync.dma_start(
+                        out=base_scales[32 * quadrant : 32 * quadrant + 4, :].bitcast(I32),
+                        in_=base_activation_scales[0, 4 * quadrant : 4 * quadrant + 4, :].bitcast(I32),
+                    )
+        xr_sb = loads.tile([P, TILES_PER_BANK, FEATURES], BF16)
+        nc.sync.dma_start(out=xr_sb[:], in_=x_rows[:, ROW_TILES - TILES_PER_BANK : ROW_TILES, :])
+        rows_loaded.append(xr_sb)
 
         identity = consts.tile([P, P], F32)
         make_identity(nc, identity[:])
-
+        minus_twice_root = consts.tile([P, P], F32)
+        nc.vector.tensor_scalar(
+            out=minus_twice_root[:], in0=identity[:], scalar1=0.0, scalar2=-2.0 * root, op0=ALU.mult, op1=ALU.add
+        )
         minus_twice_grid = consts.tile([P, GRID], F32)
         nc.vector.tensor_scalar_mul(out=minus_twice_grid[:], in0=grid_bf[:], scalar1=-2.0)
+
+        def twice_distance(unit):
+            r, g = unit // GRID, unit % GRID
+            block0 = (r % TILES_PER_BANK) * BLOCKS
+            twice_d = work.tile([P, TILE_X], F32, bufs=5)
+            nc.scalar.activation(
+                out=twice_d[:],
+                in_=quarters_loaded[r // TILES_PER_BANK][:, block0 : block0 + BLOCKS, :].rearrange("p m q -> p (m q)"),
+                func=ACT.Abs, bias=minus_twice_grid[:, g : g + 1], scale=2.0,
+            )
+            return twice_d
+
+        def transpose_plain(twice_dist):
+            turned = psum_s.tile([P, BLOCKS, P], F32, tag="turned")
+            for m in range(BLOCKS):
+                nc.tensor.transpose(turned[:, m, :], twice_dist[:, m * P : (m + 1) * P], identity[:])
+            return turned
+
+        def transpose_and_shift(twice_dist):
+            shifted = psum_s.tile([P, BLOCKS, P], F32, tag="turned")
+            for m in range(BLOCKS):
+                nc.tensor.matmul(
+                    out=shifted[:, m, :], lhsT=twice_dist[:, m * P : (m + 1) * P], rhs=identity[:],
+                    is_transpose=True, start=True, stop=False,
+                )
+                nc.tensor.matmul(
+                    out=shifted[:, m, :], lhsT=minus_twice_root[:], rhs=identity[:],
+                    is_transpose=True, start=False, stop=True,
+                )
+            return shifted
+
+        def gap_squared(turned):
+            gap_sq = work.tile([P, TILE_X], F32)
+            nc.scalar.activation(
+                out=gap_sq[:], in_=turned[:].rearrange("p m n -> p (m n)"), func=ACT.Square, bias=1.0, scale=-0.5
+            )
+            return gap_sq
+
+        def shifted_squared(shifted):
+            shifted_sq = work.tile([P, TILE_X], F32)
+            nc.scalar.activation(
+                out=shifted_sq[:], in_=shifted[:].rearrange("p m n -> p (m n)"), func=ACT.Square,
+                bias=sqrt3 * (root + beta), scale=sqrt3 / 2.0,
+            )
+            return shifted_sq
+
+        def minus_outer_piece(out_plane, turned, gap_sq):
+            nc.vector.scalar_tensor_tensor(
+                out=out_plane, in0=turned[:].rearrange("p m n -> p (m n)"), scalar=2.0, in1=gap_sq[:],
+                op0=ALU.subtract, op1=ALU.mult,
+            )
+
+        def inner_piece(out_plane, shifted, shifted_sq):
+            nc.vector.scalar_tensor_tensor(
+                out=out_plane, in0=shifted_sq[:], scalar=3.0 * gamma, in1=shifted[:].rearrange("p m n -> p (m n)"),
+                op0=ALU.add, op1=ALU.mult,
+            )
+
+        def clamped_outer(outer):
+            nc.vector.tensor_scalar(
+                out=outer[:], in0=outer[:], scalar1=-1.0, scalar2=0.0, op0=ALU.mult, op1=ALU.max
+            )
+
+        def smaller_piece(outer, inner):
+            basis = work.tile([P, GRID, TILE_X], BF16, align_bytes=64)
+            nc.vector.tensor_tensor(out=basis[:], in0=outer[:], in1=inner[:], op=ALU.min)
+            return basis
+
+        def spline_passes(basis, spline_sums, slot):
+            basis_codes = work.tile([P, GRID, P], U32, align_bytes=64)
+            basis_scales = work.tile([P, GRID, P], U8, align_bytes=64)
+            nc.vector.quantize_mx(
+                out=basis_codes[:].rearrange("p g b -> p (g b)").bitcast(FP8X4),
+                scales=basis_scales[:].rearrange("p g b -> p (g b)"),
+                in_=basis[:].rearrange("p g n -> p (g n)"),
+            )
+            for g in range(GRID):
+                nc.tensor.matmul_mx(
+                    out=spline_sums[:, slot, :],
+                    lhsT=basis_codes[:, g, :].bitcast(FP8X4),
+                    lhsT_scale=basis_scales[:, g, :],
+                    rhs=spline_codes[:, g, :].bitcast(FP8X4),
+                    rhs_scale=spline_scales[:, g, :],
+                    start=(g == 0),
+                    stop=(g == GRID - 1),
+                )
 
         def transpose_x(bank):
             x_t = psum_x.tile([P, HALVES, BANK_ROWS], F32, tag="x_t")
             for r in range(TILES_PER_BANK):
-                x_words = x_loaded[bank][:, r, :].bitcast(F32)
+                x_words = rows_loaded[bank][:, r, :].bitcast(F32)
                 for u in range(HALVES):
                     nc.tensor.transpose(
-                        x_t[:, u, r * P : (r + 1) * P],
-                        x_words[:, u : FEATURES // PAIR : HALVES],
-                        identity[:],
+                        x_t[:, u, r * P : (r + 1) * P], x_words[:, u : FEATURES // PAIR : HALVES], identity[:]
                     )
             return x_t
 
-        spline_t = psum_x.tile([P, PACK, OUTPUTS], F32, tag="x_t")
-        x_transposed = [transpose_x(0)]
-
-        spline_sorted = consts.tile([P, PACK, P], F32)
-        nc.vector.tensor_copy(
-            out=spline_sorted[:], in_=spline_sb[:].bitcast(F32).rearrange("o (p j) -> o j p", j=PACK)
-        )
-        for j in range(PACK):
-            nc.tensor.transpose(spline_t[:, j, :], spline_sorted[:, j, :], identity[:])
-        spline_grouped = consts.tile([P, GRID, OUTPUTS, PACK], BF16, align_bytes=64)
-        nc.vector.tensor_copy(
-            out=spline_grouped[:],
-            in_=spline_t[:]
-            .rearrange("p j o -> p (j o)")
-            .bitcast(BF16)
-            .rearrange("p (j o g) -> p g o j", j=PACK, g=GRID),
-        )
-        spline_codes = consts.tile([P, GRID, OUTPUTS], U32, align_bytes=64)
-        spline_scales = consts.tile([P, GRID, OUTPUTS], U8, align_bytes=64)
-        nc.vector.quantize_mx(
-            out=spline_codes[:].rearrange("p g o -> p (g o)").bitcast(FP8X4),
-            scales=spline_scales[:].rearrange("p g o -> p (g o)"),
-            in_=spline_grouped[:].rearrange("p g o t -> p (g o t)"),
-        )
-
-        for bank in range(1, BANKS):
-            x_transposed.append(transpose_x(bank))
-
-        def twice_distance(bank, first, tiles):
-            rows = tiles * P
-            x_values = (
-                x_transposed[bank][:]
-                .rearrange("p u n -> p (u n)")
-                .bitcast(BF16)
-                .rearrange("p (u n e) -> p n u e", u=HALVES, e=PAIR)[:, first * P : first * P + rows, :, :]
-            )
-            twice_dist = work.tile([P, GRID, rows * PACK], F32)
-            for g in range(GRID):
-                nc.scalar.activation(
-                    out=twice_dist[:, g, :].rearrange("p (n u e) -> p n u e", u=HALVES, e=PAIR),
-                    in_=x_values, func=ACT.Abs, bias=minus_twice_grid[:, g : g + 1], scale=2.0,
-                )
-            return twice_dist
-
-        def regroup_x(bank, first, tiles):
-            rows = tiles * P
-            x_grouped = work.tile([P, rows, PACK], BF16, align_bytes=64)
+        def regroup_x(bank, x_t, x_grouped):
+            row0 = (bank % BANKS_PER_GROUP) * BANK_ROWS
             nc.scalar.copy(
-                out=x_grouped[:].bitcast(F32),
-                in_=x_transposed[bank][:, :, first * P : first * P + rows].rearrange("p u n -> p n u"),
+                out=x_grouped[:, row0 : row0 + BANK_ROWS, :].bitcast(F32), in_=x_t[:].rearrange("p u n -> p n u")
             )
-            return x_grouped
-
-        def gap_squared(twice_dist, tiles):
-            gap_sq = work.tile([P, GRID, tiles * P * PACK], F32)
-            nc.scalar.activation(out=gap_sq[:], in_=twice_dist[:], func=ACT.Square, bias=1.0, scale=-0.5)
-            return gap_sq
-
-        def shifted_squared(twice_dist, tiles):
-            shifted_sq = work.tile([P, GRID, tiles * P * PACK], F32)
-            nc.scalar.activation(out=shifted_sq[:], in_=twice_dist[:], func=ACT.Square, bias=beta, scale=0.5)
-            return shifted_sq
-
-        def six_root_gaps(twice_dist, tiles, on_scalar):
-            root_gap = work.tile([P, GRID, tiles * P * PACK], F32)
-            if on_scalar:
-                nc.scalar.activation(
-                    out=root_gap[:], in_=twice_dist[:], func=ACT.Identity, bias=6.0 * root, scale=-3.0
-                )
-            else:
-                nc.vector.tensor_scalar(
-                    out=root_gap[:], in0=twice_dist[:], scalar1=-3.0, scalar2=6.0 * root,
-                    op0=ALU.mult, op1=ALU.add,
-                )
-            return root_gap
-
-        def minus_outer_piece(twice_dist, gap_sq, tiles):
-            minus_outer = work.tile([P, GRID, tiles * P * PACK], BF16)
-            nc.vector.scalar_tensor_tensor(
-                out=minus_outer[:], in0=twice_dist[:], scalar=2.0, in1=gap_sq[:],
-                op0=ALU.subtract, op1=ALU.mult,
-            )
-            return minus_outer
-
-        def minus_inner_piece(shifted_sq, root_gap, tiles):
-            minus_inner = work.tile([P, GRID, tiles * P * PACK], BF16)
-            nc.vector.scalar_tensor_tensor(
-                out=minus_inner[:], in0=shifted_sq[:], scalar=gamma, in1=root_gap[:],
-                op0=ALU.add, op1=ALU.mult,
-            )
-            return minus_inner
-
-        def larger_piece(minus_outer, minus_inner, tiles):
-            minus_basis = work.tile([P, GRID, tiles * P * PACK], BF16, align_bytes=64)
-            nc.vector.tensor_tensor(out=minus_basis[:], in0=minus_outer[:], in1=minus_inner[:], op=ALU.max)
-            return minus_basis
-
-        def clamp_at_zero(minus_basis):
-            nc.vector.tensor_scalar_min(out=minus_basis[:], in0=minus_basis[:], scalar1=0.0)
 
         def base_product(x_grouped, tiles):
             x_codes = work.tile([P, tiles, P], U32, align_bytes=64)
@@ -203,9 +216,9 @@ def tile_advancedkanlayer_pa_s_kernel(
             nc.vector.quantize_mx(
                 out=x_codes[:].rearrange("p r b -> p (r b)").bitcast(FP8X4),
                 scales=x_scales[:].rearrange("p r b -> p (r b)"),
-                in_=x_grouped[:].rearrange("p n t -> p (n t)"),
+                in_=x_grouped[:, : tiles * P, :].rearrange("p n t -> p (n t)"),
             )
-            base_sums = psum_out.tile([P, BANK_TILES, OUTPUTS], F32, bufs=2)
+            base_sums = psum_out.tile([P, GROUP_TILES, OUTPUTS], F32)
             for r in range(tiles):
                 nc.tensor.matmul_mx(
                     out=base_sums[:, r, :],
@@ -223,63 +236,96 @@ def tile_advancedkanlayer_pa_s_kernel(
             nc.scalar.mul(out=tenth_base[:], in_=base_sums[:, :tiles, :], mul=0.1)
             return tenth_base
 
-        def minus_spline_product(minus_basis, tiles):
-            basis_codes = work.tile([P, GRID, tiles, P], U32, align_bytes=64)
-            basis_scales = work.tile([P, GRID, tiles, P], U8, align_bytes=64)
-            nc.vector.quantize_mx(
-                out=basis_codes[:].rearrange("p g r b -> p (g r b)").bitcast(FP8X4),
-                scales=basis_scales[:].rearrange("p g r b -> p (g r b)"),
-                in_=minus_basis[:].rearrange("p g n -> p (g n)"),
-            )
-            minus_spline = psum_out.tile([P, BANK_TILES, OUTPUTS], F32)
-            for r in range(tiles):
-                for g in range(GRID):
-                    nc.tensor.matmul_mx(
-                        out=minus_spline[:, r, :],
-                        lhsT=basis_codes[:, g, r, :].bitcast(FP8X4),
-                        lhsT_scale=basis_scales[:, g, r, :],
-                        rhs=spline_codes[:, g, :].bitcast(FP8X4),
-                        rhs_scale=spline_scales[:, g, :],
-                        start=(g == 0),
-                        stop=(g == GRID - 1),
-                    )
-            return minus_spline
-
-        def subtract_and_store(bank, first, tiles, tenth_base, minus_spline):
+        def add_and_store(tile0, tiles, tenth_base, spline_sums):
+            slot0 = tile0 % GROUP_TILES
             result = work.tile([P, tiles, OUTPUTS], F32)
-            nc.vector.tensor_sub(out=result[:], in0=tenth_base[:], in1=minus_spline[:, :tiles, :])
-            tile0 = bank * TILES_PER_BANK + first
+            nc.vector.tensor_add(
+                out=result[:], in0=tenth_base[:, slot0 : slot0 + tiles, :], in1=spline_sums[:, slot0 : slot0 + tiles, :]
+            )
             nc.sync.dma_start(out=out_rows[:, tile0 : tile0 + tiles, :], in_=result[:])
 
-        chunks = CHUNKS
-        last = len(chunks) - 1
-        minus_outer, minus_inner, minus_basis = {}, {}, {}
-        base_sums, tenth_base, minus_spline = {}, {}, {}
-        for c in range(len(chunks) + 2):
-            if c >= 2:
-                tenth_base[c - 2] = a_tenth_of(base_sums[c - 2], chunks[c - 2][2])
-            if c <= last:
-                bank, first, tiles = chunks[c]
-                on_scalar = c >= SCALAR_ROOT_GAPS_FROM
-                twice_dist = twice_distance(bank, first, tiles)
-                x_grouped = regroup_x(bank, first, tiles)
-                gap_sq = gap_squared(twice_dist, tiles)
-                if on_scalar:
-                    root_gap = six_root_gaps(twice_dist, tiles, True)
-                shifted_sq = shifted_squared(twice_dist, tiles)
-            if c <= last:
-                base_sums[c] = base_product(x_grouped, tiles)
-                if not on_scalar:
-                    root_gap = six_root_gaps(twice_dist, tiles, False)
-            if 1 <= c <= last + 1:
-                minus_basis[c - 1] = larger_piece(minus_outer[c - 1], minus_inner[c - 1], chunks[c - 1][2])
-            if c <= last:
-                minus_outer[c] = minus_outer_piece(twice_dist, gap_sq, tiles)
-            if 1 <= c <= last + 1:
-                clamp_at_zero(minus_basis[c - 1])
-            if c >= 2:
-                subtract_and_store(chunks[c - 2][0], chunks[c - 2][1], chunks[c - 2][2], tenth_base[c - 2], minus_spline[c - 2])
-            if c <= last:
-                minus_inner[c] = minus_inner_piece(shifted_sq, root_gap, tiles)
-            if 1 <= c <= last + 1:
-                minus_spline[c - 1] = minus_spline_product(minus_basis[c - 1], chunks[c - 1][2])
+        twice_dist, turned, shifted = {}, {}, {}
+        for unit in range(AHEAD):
+            twice_dist[unit] = twice_distance(unit)
+            turned[unit] = transpose_plain(twice_dist[unit])
+            if unit < AHEAD - 1:
+                shifted[unit] = transpose_and_shift(twice_dist[unit])
+
+        spline_t = psum_x.tile([P, PACK, OUTPUTS], F32, tag="x_t")
+        for j in range(PACK):
+            nc.tensor.transpose(
+                spline_t[:, j, :], spline_sb[:].bitcast(F32)[:, j * QUARTER : (j + 1) * QUARTER], identity[:]
+            )
+        spline_grouped = consts.tile([P, GRID, OUTPUTS, PACK], BF16, align_bytes=64)
+        spline_codes = consts.tile([P, GRID, OUTPUTS], U32, align_bytes=64)
+        spline_scales = consts.tile([P, GRID, OUTPUTS], U8, align_bytes=64)
+
+        def regroup_spline_weight():
+            nc.vector.tensor_copy(
+                out=spline_grouped[:],
+                in_=spline_t[:]
+                .rearrange("p j o -> p (j o)")
+                .bitcast(BF16)
+                .rearrange("p (j o g) -> p g o j", j=PACK, g=GRID),
+            )
+
+        def quantise_spline_weight():
+            nc.vector.quantize_mx(
+                out=spline_codes[:].rearrange("p g o -> p (g o)").bitcast(FP8X4),
+                scales=spline_scales[:].rearrange("p g o -> p (g o)"),
+                in_=spline_grouped[:].rearrange("p g o t -> p (g o t)"),
+            )
+
+        outer, inner, basis, tenth_base = {}, {}, {}, {}
+        x_t, x_grouped, base_sums, spline_sums = None, None, None, None
+        for unit in range(UNITS + GRID):
+            r, g = unit // GRID, unit % GRID
+            before = r - 1
+            live = unit < UNITS
+
+            if g == 0 and 1 <= r <= BANKS:
+                x_t = transpose_x(r - 1)
+            if g == 1 and r in TENTH_AT:
+                group = TENTH_AT.index(r)
+                tenth_base[group] = a_tenth_of(base_sums, min(GROUP_TILES, ROW_TILES - group * GROUP_TILES))
+            if live:
+                gap_sq = gap_squared(turned[unit])
+                shifted_sq = shifted_squared(shifted[unit])
+            if unit + AHEAD < UNITS:
+                twice_dist[unit + AHEAD] = twice_distance(unit + AHEAD)
+            if g == 1 and 1 <= r <= BANKS:
+                if (r - 1) % BANKS_PER_GROUP == 0:
+                    x_grouped = work.tile([P, BANKS_PER_GROUP * BANK_ROWS, PACK], BF16, align_bytes=64)
+                regroup_x(r - 1, x_t, x_grouped)
+
+            if live:
+                if g == 0:
+                    outer[r] = work.tile([P, GRID, TILE_X], BF16, name="outer")
+                    inner[r] = work.tile([P, GRID, TILE_X], BF16, name="inner")
+                minus_outer_piece(outer[r][:, g, :], turned[unit], gap_sq)
+            if unit + AHEAD - 1 < UNITS:
+                shifted[unit + AHEAD - 1] = transpose_and_shift(twice_dist[unit + AHEAD - 1])
+            if unit == 1:
+                regroup_spline_weight()
+            if before >= 0 and g == 0:
+                clamped_outer(outer[before])
+            if before >= 0 and g == 1:
+                if before % GROUP_TILES == 0:
+                    spline_sums = psum_out.tile([P, GROUP_TILES, OUTPUTS], F32)
+                spline_passes(basis[before], spline_sums, before % GROUP_TILES)
+            if live:
+                inner_piece(inner[r][:, g, :], shifted[unit], shifted_sq)
+            if unit + AHEAD < UNITS:
+                turned[unit + AHEAD] = transpose_plain(twice_dist[unit + AHEAD])
+            if unit == 1:
+                quantise_spline_weight()
+            if before >= 0 and g == 0:
+                basis[before] = smaller_piece(outer[before], inner[before])
+                if before == ROW_TILES - 1:
+                    add_and_store(before - 1, 1, tenth_base[before // GROUP_TILES], spline_sums)
+                elif before > 0 and before % GROUP_TILES == 0:
+                    add_and_store(before - GROUP_TILES, GROUP_TILES, tenth_base[before // GROUP_TILES - 1], spline_sums)
+            if g == 1 and r in QUANTISE_X_AT:
+                group = QUANTISE_X_AT.index(r)
+                base_sums = base_product(x_grouped, min(GROUP_TILES, ROW_TILES - group * GROUP_TILES))
+        add_and_store(ROW_TILES - 1, 1, tenth_base[(ROW_TILES - 1) // GROUP_TILES], spline_sums)

@@ -30,6 +30,9 @@ PAIR = 2
 GROUP_TILES = 4
 BANKS_PER_GROUP = GROUP_TILES // TILES_PER_BANK
 AHEAD = 3
+HOLD_STORES_FROM = 2 * (UNITS - 6)
+VECTOR_REGROUPS = 1
+CHUNKS = [[0], [1], [2], [3], [4], [5], [6], [7], [8], [9]]
 QUANTISE_X_AT = [2, 4, 6]
 TENTH_AT = [4, 6, 8]
 
@@ -68,7 +71,6 @@ def tile_advancedkanlayer_pa_s_kernel(
         grid_bf = consts.tile([P, GRID], BF16)
         nc.scalar.dma_start(out=grid_bf[:], in_=grid_points.partition_broadcast(P))
         spline_sb = consts.tile([P, FEATURES * GRID], BF16)
-        nc.scalar.dma_start(out=spline_sb[:], in_=spline_weight.rearrange("o i g -> o (i g)"))
 
         base_words = consts.tile([P, 2 * OUTPUTS], U8, align_bytes=64)
         base_scales = consts.tile([P, OUTPUTS], U8, align_bytes=64)
@@ -82,6 +84,8 @@ def tile_advancedkanlayer_pa_s_kernel(
             for m in range(0, TILES_PER_BANK * BLOCKS, width):
                 block0 = bank * TILES_PER_BANK * BLOCKS + m
                 nc.sync.dma_start(out=xq_sb[:, m : m + width, :], in_=x_quarters[:, block0 : block0 + width, :])
+                if block0 == 0:
+                    nc.sync.dma_start(out=spline_sb[:], in_=spline_weight.rearrange("o i g -> o (i g)"))
             quarters_loaded.append(xq_sb)
             if bank > 0:
                 xr_sb = loads.tile([P, TILES_PER_BANK, FEATURES], BF16)
@@ -170,29 +174,30 @@ def tile_advancedkanlayer_pa_s_kernel(
                 out=outer[:], in0=outer[:], scalar1=-1.0, scalar2=0.0, op0=ALU.mult, op1=ALU.max
             )
 
-        def smaller_piece(outer, inner):
-            basis = work.tile([P, GRID, TILE_X], BF16, align_bytes=64)
+        def smaller_piece(outer, inner, tiles):
+            basis = work.tile([P, tiles, GRID, TILE_X], BF16, align_bytes=64)
             nc.vector.tensor_tensor(out=basis[:], in0=outer[:], in1=inner[:], op=ALU.min)
             return basis
 
-        def spline_passes(basis, spline_sums, slot):
-            basis_codes = work.tile([P, GRID, P], U32, align_bytes=64)
-            basis_scales = work.tile([P, GRID, P], U8, align_bytes=64)
+        def spline_passes(basis, tiles, spline_sums, slot0):
+            basis_codes = work.tile([P, tiles, GRID, P], U32, align_bytes=64)
+            basis_scales = work.tile([P, tiles, GRID, P], U8, align_bytes=64)
             nc.vector.quantize_mx(
-                out=basis_codes[:].rearrange("p g b -> p (g b)").bitcast(FP8X4),
-                scales=basis_scales[:].rearrange("p g b -> p (g b)"),
-                in_=basis[:].rearrange("p g n -> p (g n)"),
+                out=basis_codes[:].rearrange("p r g b -> p (r g b)").bitcast(FP8X4),
+                scales=basis_scales[:].rearrange("p r g b -> p (r g b)"),
+                in_=basis[:].rearrange("p r g n -> p (r g n)"),
             )
-            for g in range(GRID):
-                nc.tensor.matmul_mx(
-                    out=spline_sums[:, slot, :],
-                    lhsT=basis_codes[:, g, :].bitcast(FP8X4),
-                    lhsT_scale=basis_scales[:, g, :],
-                    rhs=spline_codes[:, g, :].bitcast(FP8X4),
-                    rhs_scale=spline_scales[:, g, :],
-                    start=(g == 0),
-                    stop=(g == GRID - 1),
-                )
+            for t in range(tiles):
+                for g in range(GRID):
+                    nc.tensor.matmul_mx(
+                        out=spline_sums[:, slot0 + t, :],
+                        lhsT=basis_codes[:, t, g, :].bitcast(FP8X4),
+                        lhsT_scale=basis_scales[:, t, g, :],
+                        rhs=spline_codes[:, g, :].bitcast(FP8X4),
+                        rhs_scale=spline_scales[:, g, :],
+                        start=(g == 0),
+                        stop=(g == GRID - 1),
+                    )
 
         def transpose_x(bank):
             x_t = psum_x.tile([P, HALVES, BANK_ROWS], F32, tag="x_t")
@@ -206,9 +211,14 @@ def tile_advancedkanlayer_pa_s_kernel(
 
         def regroup_x(bank, x_t, x_grouped):
             row0 = (bank % BANKS_PER_GROUP) * BANK_ROWS
-            nc.scalar.copy(
-                out=x_grouped[:, row0 : row0 + BANK_ROWS, :].bitcast(F32), in_=x_t[:].rearrange("p u n -> p n u")
-            )
+            if bank < VECTOR_REGROUPS:
+                nc.vector.tensor_copy(
+                    out=x_grouped[:, row0 : row0 + BANK_ROWS, :].bitcast(F32), in_=x_t[:].rearrange("p u n -> p n u")
+                )
+            else:
+                nc.scalar.copy(
+                    out=x_grouped[:, row0 : row0 + BANK_ROWS, :].bitcast(F32), in_=x_t[:].rearrange("p u n -> p n u")
+                )
 
         def base_product(x_grouped, tiles):
             x_codes = work.tile([P, tiles, P], U32, align_bytes=64)
@@ -244,6 +254,27 @@ def tile_advancedkanlayer_pa_s_kernel(
             )
             nc.sync.dma_start(out=out_rows[:, tile0 : tile0 + tiles, :], in_=result[:])
 
+        spline_t = psum_x.tile([P, PACK, OUTPUTS], F32, tag="x_t")
+        for j in range(PACK):
+            nc.tensor.transpose(
+                spline_t[:, j, :], spline_sb[:].bitcast(F32)[:, j * QUARTER : (j + 1) * QUARTER], identity[:]
+            )
+        spline_grouped = consts.tile([P, GRID, OUTPUTS, PACK], BF16, align_bytes=64)
+        nc.vector.tensor_copy(
+            out=spline_grouped[:],
+            in_=spline_t[:]
+            .rearrange("p j o -> p (j o)")
+            .bitcast(BF16)
+            .rearrange("p (j o g) -> p g o j", j=PACK, g=GRID),
+        )
+        spline_codes = consts.tile([P, GRID, OUTPUTS], U32, align_bytes=64)
+        spline_scales = consts.tile([P, GRID, OUTPUTS], U8, align_bytes=64)
+        nc.vector.quantize_mx(
+            out=spline_codes[:].rearrange("p g o -> p (g o)").bitcast(FP8X4),
+            scales=spline_scales[:].rearrange("p g o -> p (g o)"),
+            in_=spline_grouped[:].rearrange("p g o t -> p (g o t)"),
+        )
+
         twice_dist, turned, shifted = {}, {}, {}
         for unit in range(AHEAD):
             twice_dist[unit] = twice_distance(unit)
@@ -251,46 +282,59 @@ def tile_advancedkanlayer_pa_s_kernel(
             if unit < AHEAD - 1:
                 shifted[unit] = transpose_and_shift(twice_dist[unit])
 
-        spline_t = psum_x.tile([P, PACK, OUTPUTS], F32, tag="x_t")
-        for j in range(PACK):
-            nc.tensor.transpose(
-                spline_t[:, j, :], spline_sb[:].bitcast(F32)[:, j * QUARTER : (j + 1) * QUARTER], identity[:]
-            )
-        spline_grouped = consts.tile([P, GRID, OUTPUTS, PACK], BF16, align_bytes=64)
-        spline_codes = consts.tile([P, GRID, OUTPUTS], U32, align_bytes=64)
-        spline_scales = consts.tile([P, GRID, OUTPUTS], U8, align_bytes=64)
+        chunk_of = {}
+        for chunk in CHUNKS:
+            for tile in chunk:
+                chunk_of[tile] = chunk
+        outer, inner, tenth_base = {}, {}, {}
+        x_t, x_grouped, base_sums, spline_sums, basis = None, None, None, None, None
+        steps, stores = [], []
+        sums = {}
+        place = 0
 
-        def regroup_spline_weight():
-            nc.vector.tensor_copy(
-                out=spline_grouped[:],
-                in_=spline_t[:]
-                .rearrange("p j o -> p (j o)")
-                .bitcast(BF16)
-                .rearrange("p (j o g) -> p g o j", j=PACK, g=GRID),
+        def one_step(place, spline_sums, basis):
+            opens_bank = (
+                bool(steps) and steps[0][0] == "multiply" and steps[0][1][0] % GROUP_TILES == 0
+                and steps[0][1][0] // GROUP_TILES < ROW_TILES // GROUP_TILES
             )
+            if steps and not (opens_bank and stores):
+                kind, chunk = steps[0]
+                steps.remove(steps[0])
+                first = chunk[0]
+                if kind == "clamp":
+                    clamped_outer(outer[first])
+                if kind == "choose":
+                    basis = smaller_piece(outer[first], inner[first], len(chunk))
+                if kind == "multiply":
+                    if first // GROUP_TILES == ROW_TILES // GROUP_TILES and first % GROUP_TILES == 0:
+                        sums[first // GROUP_TILES] = psum_s.tile([P, GROUP_TILES, OUTPUTS], F32, name="last_sums", tag="turned")
+                    elif first % GROUP_TILES == 0:
+                        sums[first // GROUP_TILES] = psum_out.tile([P, GROUP_TILES, OUTPUTS], F32, name="spline_sums")
+                    spline_sums = sums[first // GROUP_TILES]
+                    spline_passes(basis, len(chunk), spline_sums, first % GROUP_TILES)
+                    stores.append((place + 2, chunk))
+            elif stores and (opens_bank or stores[0][0] <= place < HOLD_STORES_FROM or place >= GRID * UNITS):
+                chunk = stores[0][1]
+                stores.remove(stores[0])
+                first, done = chunk[0], chunk[-1] + 1
+                if first // GROUP_TILES == ROW_TILES // GROUP_TILES:
+                    add_and_store(first, len(chunk), tenth_base[first // GROUP_TILES], sums[first // GROUP_TILES])
+                elif done % GROUP_TILES == 0:
+                    add_and_store(done - GROUP_TILES, GROUP_TILES, tenth_base[first // GROUP_TILES], sums[first // GROUP_TILES])
+            return spline_sums, basis
 
-        def quantise_spline_weight():
-            nc.vector.quantize_mx(
-                out=spline_codes[:].rearrange("p g o -> p (g o)").bitcast(FP8X4),
-                scales=spline_scales[:].rearrange("p g o -> p (g o)"),
-                in_=spline_grouped[:].rearrange("p g o t -> p (g o t)"),
-            )
-
-        outer, inner, basis, tenth_base = {}, {}, {}, {}
-        x_t, x_grouped, base_sums, spline_sums = None, None, None, None
-        for unit in range(UNITS + GRID):
+        for unit in range(UNITS):
             r, g = unit // GRID, unit % GRID
-            before = r - 1
-            live = unit < UNITS
+            chunk = chunk_of[r]
+            first = chunk[0]
 
             if g == 0 and 1 <= r <= BANKS:
                 x_t = transpose_x(r - 1)
             if g == 1 and r in TENTH_AT:
                 group = TENTH_AT.index(r)
                 tenth_base[group] = a_tenth_of(base_sums, min(GROUP_TILES, ROW_TILES - group * GROUP_TILES))
-            if live:
-                gap_sq = gap_squared(turned[unit])
-                shifted_sq = shifted_squared(shifted[unit])
+            gap_sq = gap_squared(turned[unit])
+            shifted_sq = shifted_squared(shifted[unit])
             if unit + AHEAD < UNITS:
                 twice_dist[unit + AHEAD] = twice_distance(unit + AHEAD)
             if g == 1 and 1 <= r <= BANKS:
@@ -298,34 +342,24 @@ def tile_advancedkanlayer_pa_s_kernel(
                     x_grouped = work.tile([P, BANKS_PER_GROUP * BANK_ROWS, PACK], BF16, align_bytes=64)
                 regroup_x(r - 1, x_t, x_grouped)
 
-            if live:
-                if g == 0:
-                    outer[r] = work.tile([P, GRID, TILE_X], BF16, name="outer")
-                    inner[r] = work.tile([P, GRID, TILE_X], BF16, name="inner")
-                minus_outer_piece(outer[r][:, g, :], turned[unit], gap_sq)
+            if r == first and g == 0:
+                outer[first] = work.tile([P, len(chunk), GRID, TILE_X], BF16, name="outer")
+                inner[first] = work.tile([P, len(chunk), GRID, TILE_X], BF16, name="inner")
+            minus_outer_piece(outer[first][:, r - first, g, :], turned[unit], gap_sq)
             if unit + AHEAD - 1 < UNITS:
                 shifted[unit + AHEAD - 1] = transpose_and_shift(twice_dist[unit + AHEAD - 1])
-            if unit == 1:
-                regroup_spline_weight()
-            if before >= 0 and g == 0:
-                clamped_outer(outer[before])
-            if before >= 0 and g == 1:
-                if before % GROUP_TILES == 0:
-                    spline_sums = psum_out.tile([P, GROUP_TILES, OUTPUTS], F32)
-                spline_passes(basis[before], spline_sums, before % GROUP_TILES)
-            if live:
-                inner_piece(inner[r][:, g, :], shifted[unit], shifted_sq)
+            spline_sums, basis = one_step(place, spline_sums, basis)
+            place += 1
+            inner_piece(inner[first][:, r - first, g, :], shifted[unit], shifted_sq)
             if unit + AHEAD < UNITS:
                 turned[unit + AHEAD] = transpose_plain(twice_dist[unit + AHEAD])
-            if unit == 1:
-                quantise_spline_weight()
-            if before >= 0 and g == 0:
-                basis[before] = smaller_piece(outer[before], inner[before])
-                if before == ROW_TILES - 1:
-                    add_and_store(before - 1, 1, tenth_base[before // GROUP_TILES], spline_sums)
-                elif before > 0 and before % GROUP_TILES == 0:
-                    add_and_store(before - GROUP_TILES, GROUP_TILES, tenth_base[before // GROUP_TILES - 1], spline_sums)
+            spline_sums, basis = one_step(place, spline_sums, basis)
+            place += 1
+            if r == chunk[-1] and g == GRID - 1:
+                steps.extend([("clamp", chunk), ("choose", chunk), ("multiply", chunk)])
             if g == 1 and r in QUANTISE_X_AT:
                 group = QUANTISE_X_AT.index(r)
                 base_sums = base_product(x_grouped, min(GROUP_TILES, ROW_TILES - group * GROUP_TILES))
-        add_and_store(ROW_TILES - 1, 1, tenth_base[(ROW_TILES - 1) // GROUP_TILES], spline_sums)
+        while steps or stores:
+            spline_sums, basis = one_step(place, spline_sums, basis)
+            place += 1

@@ -30,6 +30,7 @@ PAIR = 2
 GROUP_TILES = 4
 BANKS_PER_GROUP = GROUP_TILES // TILES_PER_BANK
 AHEAD = 3
+WARM_UP_MATMULS = 4
 HOLD_STORES_FROM = 2 * (UNITS - 6)
 VECTOR_REGROUPS = 1
 CHUNKS = [[0], [1], [2], [3], [4], [5], [6], [7], [8], [9]]
@@ -254,6 +255,9 @@ def tile_advancedkanlayer_pa_s_kernel(
             )
             nc.sync.dma_start(out=out_rows[:, tile0 : tile0 + tiles, :], in_=result[:])
 
+        warm_up = psum_out.tile([P, GROUP_TILES, OUTPUTS], F32, name="spline_sums")
+        for turn in range(WARM_UP_MATMULS):
+            nc.tensor.matmul(out=warm_up[:, 0, :], lhsT=identity[:], rhs=identity[:], start=True, stop=True)
         spline_t = psum_x.tile([P, PACK, OUTPUTS], F32, tag="x_t")
         for j in range(PACK):
             nc.tensor.transpose(

@@ -32,6 +32,7 @@ BANKS_PER_GROUP = GROUP_TILES // TILES_PER_BANK
 AHEAD = 3
 WARM_UP_MATMULS = 4
 HOLD_STORES_FROM = 2 * (UNITS - 6)
+SCALAR_CLAMPS_FROM = 9
 VECTOR_REGROUPS = 1
 CHUNKS = [[0], [1], [2], [3], [4], [5], [6], [7], [8], [9]]
 QUANTISE_X_AT = [2, 4, 6]
@@ -54,7 +55,7 @@ def tile_advancedkanlayer_pa_s_kernel(
     root = real_root_of_inner_piece()
     beta = (root - 1.0) / 2.0
     gamma = (root - 1.0) * (3.0 * root + 1.0) / 4.0
-    sqrt3 = 3.0**0.5
+    sqrt6 = 6.0**0.5
 
     x_quarters = x_norm.rearrange("(m n) (j q) -> (n j) m q", n=BLOCK_ROWS, j=PACK)
     x_rows = x_norm.rearrange("(r p) i -> p r i", p=P)
@@ -108,10 +109,8 @@ def tile_advancedkanlayer_pa_s_kernel(
         make_identity(nc, identity[:])
         minus_twice_root = consts.tile([P, P], F32)
         nc.vector.tensor_scalar(
-            out=minus_twice_root[:], in0=identity[:], scalar1=0.0, scalar2=-2.0 * root, op0=ALU.mult, op1=ALU.add
+            out=minus_twice_root[:], in0=identity[:], scalar1=0.0, scalar2=-root, op0=ALU.mult, op1=ALU.add
         )
-        minus_twice_grid = consts.tile([P, GRID], F32)
-        nc.vector.tensor_scalar_mul(out=minus_twice_grid[:], in0=grid_bf[:], scalar1=-2.0)
 
         def twice_distance(unit):
             r, g = unit // GRID, unit % GRID
@@ -120,7 +119,7 @@ def tile_advancedkanlayer_pa_s_kernel(
             nc.scalar.activation(
                 out=twice_d[:],
                 in_=quarters_loaded[r // TILES_PER_BANK][:, block0 : block0 + BLOCKS, :].rearrange("p m q -> p (m q)"),
-                func=ACT.Abs, bias=minus_twice_grid[:, g : g + 1], scale=2.0,
+                func=ACT.Abs, bias=grid_bf[:, g : g + 1], scale=-1.0,
             )
             return twice_d
 
@@ -146,7 +145,7 @@ def tile_advancedkanlayer_pa_s_kernel(
         def gap_squared(turned):
             gap_sq = work.tile([P, TILE_X], F32)
             nc.scalar.activation(
-                out=gap_sq[:], in_=turned[:].rearrange("p m n -> p (m n)"), func=ACT.Square, bias=1.0, scale=-0.5
+                out=gap_sq[:], in_=turned[:].rearrange("p m n -> p (m n)"), func=ACT.Square, bias=1.0, scale=-1.0
             )
             return gap_sq
 
@@ -154,25 +153,35 @@ def tile_advancedkanlayer_pa_s_kernel(
             shifted_sq = work.tile([P, TILE_X], F32)
             nc.scalar.activation(
                 out=shifted_sq[:], in_=shifted[:].rearrange("p m n -> p (m n)"), func=ACT.Square,
-                bias=sqrt3 * (root + beta), scale=sqrt3 / 2.0,
+                bias=sqrt6 * (root + beta), scale=sqrt6,
             )
             return shifted_sq
 
         def minus_outer_piece(out_plane, turned, gap_sq):
             nc.vector.scalar_tensor_tensor(
-                out=out_plane, in0=turned[:].rearrange("p m n -> p (m n)"), scalar=2.0, in1=gap_sq[:],
+                out=out_plane, in0=turned[:].rearrange("p m n -> p (m n)"), scalar=1.0, in1=gap_sq[:],
                 op0=ALU.subtract, op1=ALU.mult,
             )
 
+        def clamped_gap(turned):
+            gap = work.tile([P, TILE_X], F32)
+            nc.scalar.activation(
+                out=gap[:], in_=turned[:].rearrange("p m n -> p (m n)"), func=ACT.Relu, bias=2.0, scale=-2.0
+            )
+            return gap
+
+        def outer_piece(out_plane, gap, gap_sq):
+            nc.vector.tensor_tensor(out=out_plane, in0=gap[:], in1=gap_sq[:], op=ALU.mult)
+
         def inner_piece(out_plane, shifted, shifted_sq):
             nc.vector.scalar_tensor_tensor(
-                out=out_plane, in0=shifted_sq[:], scalar=3.0 * gamma, in1=shifted[:].rearrange("p m n -> p (m n)"),
+                out=out_plane, in0=shifted_sq[:], scalar=6.0 * gamma, in1=shifted[:].rearrange("p m n -> p (m n)"),
                 op0=ALU.add, op1=ALU.mult,
             )
 
         def clamped_outer(outer):
             nc.vector.tensor_scalar(
-                out=outer[:], in0=outer[:], scalar1=-1.0, scalar2=0.0, op0=ALU.mult, op1=ALU.max
+                out=outer[:], in0=outer[:], scalar1=-2.0, scalar2=0.0, op0=ALU.mult, op1=ALU.max
             )
 
         def smaller_piece(outer, inner, tiles):
@@ -338,6 +347,8 @@ def tile_advancedkanlayer_pa_s_kernel(
                 group = TENTH_AT.index(r)
                 tenth_base[group] = a_tenth_of(base_sums, min(GROUP_TILES, ROW_TILES - group * GROUP_TILES))
             gap_sq = gap_squared(turned[unit])
+            if r >= SCALAR_CLAMPS_FROM:
+                gap = clamped_gap(turned[unit])
             shifted_sq = shifted_squared(shifted[unit])
             if unit + AHEAD < UNITS:
                 twice_dist[unit + AHEAD] = twice_distance(unit + AHEAD)
@@ -349,7 +360,10 @@ def tile_advancedkanlayer_pa_s_kernel(
             if r == first and g == 0:
                 outer[first] = work.tile([P, len(chunk), GRID, TILE_X], BF16, name="outer")
                 inner[first] = work.tile([P, len(chunk), GRID, TILE_X], BF16, name="inner")
-            minus_outer_piece(outer[first][:, r - first, g, :], turned[unit], gap_sq)
+            if r >= SCALAR_CLAMPS_FROM:
+                outer_piece(outer[first][:, r - first, g, :], gap, gap_sq)
+            else:
+                minus_outer_piece(outer[first][:, r - first, g, :], turned[unit], gap_sq)
             if unit + AHEAD - 1 < UNITS:
                 shifted[unit + AHEAD - 1] = transpose_and_shift(twice_dist[unit + AHEAD - 1])
             spline_sums, basis = one_step(place, spline_sums, basis)
@@ -360,7 +374,9 @@ def tile_advancedkanlayer_pa_s_kernel(
             spline_sums, basis = one_step(place, spline_sums, basis)
             place += 1
             if r == chunk[-1] and g == GRID - 1:
-                steps.extend([("clamp", chunk), ("choose", chunk), ("multiply", chunk)])
+                if r < SCALAR_CLAMPS_FROM:
+                    steps.append(("clamp", chunk))
+                steps.extend([("choose", chunk), ("multiply", chunk)])
             if g == 1 and r in QUANTISE_X_AT:
                 group = QUANTISE_X_AT.index(r)
                 base_sums = base_product(x_grouped, min(GROUP_TILES, ROW_TILES - group * GROUP_TILES))

from contextlib import ExitStack

import concourse.mybir as mybir
from concourse.masks import make_identity

F32 = mybir.dt.float32
BF16 = mybir.dt.bfloat16
I32 = mybir.dt.int32
U32 = mybir.dt.uint32
U8 = mybir.dt.uint8
FP8X4 = mybir.dt.float8_e4m3fn_x4
FP4X4 = mybir.dt.float4_e2m1fn_x4
ACT = mybir.ActivationFunctionType
ALU = mybir.AluOpType

P = 128
PACK = 4
BATCH, FEATURES, OUTPUTS, GRID = 1280, 512, 128, 2
ROW_TILES = BATCH // P
UNITS = ROW_TILES * GRID
QUARTER = FEATURES // PACK
BLOCK_ROWS = P // PACK
BLOCKS = P // BLOCK_ROWS
TILE_X = P * PACK
TILES_PER_BANK = 2
BANKS = ROW_TILES // TILES_PER_BANK
BANK_ROWS = TILES_PER_BANK * P
HALVES = 2
PAIR = 2
GROUP_TILES = 4
BANKS_PER_GROUP = GROUP_TILES // TILES_PER_BANK
AHEAD = 3
WARM_UP_MATMULS = 4
HOLD_STORES_FROM = 2 * (UNITS - 6)
SCALAR_CLAMPS_FROM = 9
VECTOR_REGROUPS = 1
CHUNKS = [[0], [1], [2], [3], [4], [5], [6], [7], [8], [9]]
QUANTISE_X_AT = [2, 4, 6]
TENTH_AT = [4, 6, 8]

FLOPS = 2 * BATCH * OUTPUTS * (FEATURES * GRID + FEATURES)


def real_root_of_inner_piece():
    root = -0.3
    for step in range(60):
        root = root - (6.0 * root**3 - 6.0 * root**2 + 1.0) / (18.0 * root**2 - 12.0 * root)
    return root


def tile_advancedkanlayer_pa_s_kernel(
    tc, x_norm, spline_weight, base_activation_words, base_activation_scales, grid_points, out
):
    nc = tc.nc
    root = real_root_of_inner_piece()
    beta = (root - 1.0) / 2.0
    gamma = (root - 1.0) * (3.0 * root + 1.0) / 4.0
    sqrt6 = 6.0**0.5

    x_quarters = x_norm.rearrange("(m n) (j q) -> (n j) m q", n=BLOCK_ROWS, j=PACK)
    x_rows = x_norm.rearrange("(r p) i -> p r i", p=P)
    out_rows = out.rearrange("(r p) o -> p r o", p=P)

    with ExitStack() as stack:
        consts = stack.enter_context(tc.tile_pool(name="consts", bufs=1))
        loads = stack.enter_context(tc.tile_pool(name="loads", bufs=BANKS))
        work = stack.enter_context(tc.tile_pool(name="work", bufs=3))
        psum_s = stack.enter_context(tc.psum_pool(name="psum_s", bufs=5))
        psum_x = stack.enter_context(tc.psum_pool(name="psum_x", bufs=1))
        psum_out = stack.enter_context(tc.psum_pool(name="psum_out", bufs=1))
        stack.enter_context(tc.manual_schedule())

        grid_bf = consts.tile([P, GRID], BF16)
        nc.scalar.dma_start(out=grid_bf[:], in_=grid_points.partition_broadcast(P))
        spline_sb = consts.tile([P, FEATURES * GRID], BF16)

        base_words = consts.tile([P, 2 * OUTPUTS], U8, align_bytes=64)
        base_scales = consts.tile([P, OUTPUTS], U8, align_bytes=64)
        nc.vector.memset(base_scales[:].bitcast(I32), 0)

        quarters_loaded, rows_loaded = [], []
        for bank in range(BANKS):
            xq_sb = loads.tile([P, TILES_PER_BANK * BLOCKS, QUARTER], BF16)
            pieces = TILES_PER_BANK if bank == 0 else 1
            width = TILES_PER_BANK * BLOCKS // pieces
            for m in range(0, TILES_PER_BANK * BLOCKS, width):
                block0 = bank * TILES_PER_BANK * BLOCKS + m
                nc.sync.dma_start(out=xq_sb[:, m : m + width, :], in_=x_quarters[:, block0 : block0 + width, :])
                if block0 == 0:
                    nc.sync.dma_start(out=spline_sb[:], in_=spline_weight.rearrange("o i g -> o (i g)"))
            quarters_loaded.append(xq_sb)
            if bank > 0:
                xr_sb = loads.tile([P, TILES_PER_BANK, FEATURES], BF16)
                tile0 = (bank - 1) * TILES_PER_BANK
                nc.sync.dma_start(out=xr_sb[:], in_=x_rows[:, tile0 : tile0 + TILES_PER_BANK, :])
                rows_loaded.append(xr_sb)
            if bank == 1:
                nc.sync.dma_start(out=base_words[:].bitcast(I32), in_=base_activation_words[0].bitcast(I32))
                for quadrant in range(4):
                    nc.sync.dma_start(
                        out=base_scales[32 * quadrant : 32 * quadrant + 4, :].bitcast(I32),
                        in_=base_activation_scales[0, 4 * quadrant : 4 * quadrant + 4, :].bitcast(I32),
                    )
        xr_sb = loads.tile([P, TILES_PER_BANK, FEATURES], BF16)
        nc.sync.dma_start(out=xr_sb[:], in_=x_rows[:, ROW_TILES - TILES_PER_BANK : ROW_TILES, :])
        rows_loaded.append(xr_sb)

        identity = consts.tile([P, P], F32)
        make_identity(nc, identity[:])
        minus_twice_root = consts.tile([P, P], F32)
        nc.vector.tensor_scalar(
            out=minus_twice_root[:], in0=identity[:], scalar1=0.0, scalar2=-root, op0=ALU.mult, op1=ALU.add
        )

        def twice_distance(unit):
            r, g = unit // GRID, unit % GRID
            block0 = (r % TILES_PER_BANK) * BLOCKS
            twice_d = work.tile([P, TILE_X], F32, bufs=5)
            nc.scalar.activation(
                out=twice_d[:],
                in_=quarters_loaded[r // TILES_PER_BANK][:, block0 : block0 + BLOCKS, :].rearrange("p m q -> p (m q)"),
                func=ACT.Abs, bias=grid_bf[:, g : g + 1], scale=-1.0,
            )
            return twice_d

        def transpose_plain(twice_dist):
            turned = psum_s.tile([P, BLOCKS, P], F32, tag="turned")
            for m in range(BLOCKS):
                nc.tensor.transpose(turned[:, m, :], twice_dist[:, m * P : (m + 1) * P], identity[:])
            return turned

        def transpose_and_shift(twice_dist):
            shifted = psum_s.tile([P, BLOCKS, P], F32, tag="turned")
            for m in range(BLOCKS):
                nc.tensor.matmul(
                    out=shifted[:, m, :], lhsT=twice_dist[:, m * P : (m + 1) * P], rhs=identity[:],
                    is_transpose=True, start=True, stop=False,
                )
                nc.tensor.matmul(
                    out=shifted[:, m, :], lhsT=minus_twice_root[:], rhs=identity[:],
                    is_transpose=True, start=False, stop=True,
                )
            return shifted

        def gap_squared(turned):
            gap_sq = work.tile([P, TILE_X], F32)
            nc.scalar.activation(
                out=gap_sq[:], in_=turned[:].rearrange("p m n -> p (m n)"), func=ACT.Square, bias=1.0, scale=-1.0
            )
            return gap_sq

        def shifted_squared(shifted):
            shifted_sq = work.tile([P, TILE_X], F32)
            nc.scalar.activation(
                out=shifted_sq[:], in_=shifted[:].rearrange("p m n -> p (m n)"), func=ACT.Square,
                bias=sqrt6 * (root + beta), scale=sqrt6,
            )
            return shifted_sq

        def minus_outer_piece(out_plane, turned, gap_sq):
            nc.vector.scalar_tensor_tensor(
                out=out_plane, in0=turned[:].rearrange("p m n -> p (m n)"), scalar=1.0, in1=gap_sq[:],
                op0=ALU.subtract, op1=ALU.mult,
            )

        def clamped_gap(turned):
            gap = work.tile([P, TILE_X], F32)
            nc.scalar.activation(
                out=gap[:], in_=turned[:].rearrange("p m n -> p (m n)"), func=ACT.Relu, bias=2.0, scale=-2.0
            )
            return gap

        def outer_piece(out_plane, gap, gap_sq):
            nc.vector.tensor_tensor(out=out_plane, in0=gap[:], in1=gap_sq[:], op=ALU.mult)

        def inner_piece(out_plane, shifted, shifted_sq):
            nc.vector.scalar_tensor_tensor(
                out=out_plane, in0=shifted_sq[:], scalar=6.0 * gamma, in1=shifted[:].rearrange("p m n -> p (m n)"),
                op0=ALU.add, op1=ALU.mult,
            )

        def clamped_outer(outer):
            nc.vector.tensor_scalar(
                out=outer[:], in0=outer[:], scalar1=-2.0, scalar2=0.0, op0=ALU.mult, op1=ALU.max
            )

        def smaller_piece(outer, inner, tiles):
            basis = work.tile([P, tiles, GRID, TILE_X], BF16, align_bytes=64)
            nc.vector.tensor_tensor(out=basis[:], in0=outer[:], in1=inner[:], op=ALU.min)
            return basis

        def spline_passes(basis, tiles, spline_sums, slot0):
            basis_codes = work.tile([P, tiles, GRID, P], U32, align_bytes=64)
            basis_scales = work.tile([P, tiles, GRID, P], U8, align_bytes=64)
            nc.vector.quantize_mx(
                out=basis_codes[:].rearrange("p r g b -> p (r g b)").bitcast(FP8X4),
                scales=basis_scales[:].rearrange("p r g b -> p (r g b)"),
                in_=basis[:].rearrange("p r g n -> p (r g n)"),
            )
            for t in range(tiles):
                for g in range(GRID):
                    nc.tensor.matmul_mx(
                        out=spline_sums[:, slot0 + t, :],
                        lhsT=basis_codes[:, t, g, :].bitcast(FP8X4),
                        lhsT_scale=basis_scales[:, t, g, :],
                        rhs=spline_codes[:, g, :].bitcast(FP8X4),
                        rhs_scale=spline_scales[:, g, :],
                        start=(g == 0),
                        stop=(g == GRID - 1),
                    )

        def transpose_x(bank):
            x_t = psum_x.tile([P, HALVES, BANK_ROWS], F32, tag="x_t")
            for r in range(TILES_PER_BANK):
                x_words = rows_loaded[bank][:, r, :].bitcast(F32)
                for u in range(HALVES):
                    nc.tensor.transpose(
                        x_t[:, u, r * P : (r + 1) * P], x_words[:, u : FEATURES // PAIR : HALVES], identity[:]
                    )
            return x_t

        def regroup_x(bank, x_t, x_grouped):
            row0 = (bank % BANKS_PER_GROUP) * BANK_ROWS
            if bank < VECTOR_REGROUPS:
                nc.vector.tensor_copy(
                    out=x_grouped[:, row0 : row0 + BANK_ROWS, :].bitcast(F32), in_=x_t[:].rearrange("p u n -> p n u")
                )
            else:
                nc.scalar.copy(
                    out=x_grouped[:, row0 : row0 + BANK_ROWS, :].bitcast(F32), in_=x_t[:].rearrange("p u n -> p n u")
                )

        def base_product(x_grouped, tiles):
            x_codes = work.tile([P, tiles, P], U32, align_bytes=64)
            x_scales = work.tile([P, tiles, P], U8, align_bytes=64)
            nc.vector.quantize_mx(
                out=x_codes[:].rearrange("p r b -> p (r b)").bitcast(FP8X4),
                scales=x_scales[:].rearrange("p r b -> p (r b)"),
                in_=x_grouped[:, : tiles * P, :].rearrange("p n t -> p (n t)"),
            )
            base_sums = psum_out.tile([P, GROUP_TILES, OUTPUTS], F32)
            for r in range(tiles):
                nc.tensor.matmul_mx(
                    out=base_sums[:, r, :],
                    lhsT=x_codes[:, r, :].bitcast(FP8X4),
                    lhsT_scale=x_scales[:, r, :],
                    rhs=base_words[:].bitcast(FP4X4),
                    rhs_scale=base_scales[:],
                    start=True,
                    stop=True,
                )
            return base_sums

        def a_tenth_of(base_sums, tiles):
            tenth_base = work.tile([P, tiles, OUTPUTS], F32)
            nc.scalar.mul(out=tenth_base[:], in_=base_sums[:, :tiles, :], mul=0.1)
            return tenth_base

        def add_and_store(tile0, tiles, tenth_base, spline_sums):
            slot0 = tile0 % GROUP_TILES
            result = work.tile([P, tiles, OUTPUTS], F32)
            nc.vector.tensor_add(
                out=result[:], in0=tenth_base[:, slot0 : slot0 + tiles, :], in1=spline_sums[:, slot0 : slot0 + tiles, :]
            )
            nc.sync.dma_start(out=out_rows[:, tile0 : tile0 + tiles, :], in_=result[:])

        warm_up = psum_out.tile([P, GROUP_TILES, OUTPUTS], F32, name="spline_sums")
        for turn in range(WARM_UP_MATMULS):
            nc.tensor.matmul(out=warm_up[:, 0, :], lhsT=identity[:], rhs=identity[:], start=True, stop=True)
        spline_t = psum_x.tile([P, PACK, OUTPUTS], F32, tag="x_t")
        for j in range(PACK):
            nc.tensor.transpose(
                spline_t[:, j, :], spline_sb[:].bitcast(F32)[:, j * QUARTER : (j + 1) * QUARTER], identity[:]
            )
        spline_grouped = consts.tile([P, GRID, OUTPUTS, PACK], BF16, align_bytes=64)
        nc.vector.tensor_copy(
            out=spline_grouped[:],
            in_=spline_t[:]
            .rearrange("p j o -> p (j o)")
            .bitcast(BF16)
            .rearrange("p (j o g) -> p g o j", j=PACK, g=GRID),
        )
        spline_codes = consts.tile([P, GRID, OUTPUTS], U32, align_bytes=64)
        spline_scales = consts.tile([P, GRID, OUTPUTS], U8, align_bytes=64)
        nc.vector.quantize_mx(
            out=spline_codes[:].rearrange("p g o -> p (g o)").bitcast(FP8X4),
            scales=spline_scales[:].rearrange("p g o -> p (g o)"),
            in_=spline_grouped[:].rearrange("p g o t -> p (g o t)"),
        )

        twice_dist, turned, shifted = {}, {}, {}
        for unit in range(AHEAD):
            twice_dist[unit] = twice_distance(unit)
            turned[unit] = transpose_plain(twice_dist[unit])
            if unit < AHEAD - 1:
                shifted[unit] = transpose_and_shift(twice_dist[unit])

        chunk_of = {}
        for chunk in CHUNKS:
            for tile in chunk:
                chunk_of[tile] = chunk
        outer, inner, tenth_base = {}, {}, {}
        x_t, x_grouped, base_sums, spline_sums, basis = None, None, None, None, None
        steps, stores = [], []
        sums = {}
        place = 0

        def one_step(place, spline_sums, basis):
            opens_bank = (
                bool(steps) and steps[0][0] == "multiply" and steps[0][1][0] % GROUP_TILES == 0
                and steps[0][1][0] // GROUP_TILES < ROW_TILES // GROUP_TILES
            )
            if steps and not (opens_bank and stores):
                kind, chunk = steps[0]
                steps.remove(steps[0])
                first = chunk[0]
                if kind == "clamp":
                    clamped_outer(outer[first])
                if kind == "choose":
                    basis = smaller_piece(outer[first], inner[first], len(chunk))
                if kind == "multiply":
                    if first // GROUP_TILES == ROW_TILES // GROUP_TILES and first % GROUP_TILES == 0:
                        sums[first // GROUP_TILES] = psum_s.tile([P, GROUP_TILES, OUTPUTS], F32, name="last_sums", tag="turned")
                    elif first % GROUP_TILES == 0:
                        sums[first // GROUP_TILES] = psum_out.tile([P, GROUP_TILES, OUTPUTS], F32, name="spline_sums")
                    spline_sums = sums[first // GROUP_TILES]
                    spline_passes(basis, len(chunk), spline_sums, first % GROUP_TILES)
                    stores.append((place + 2, chunk))
            elif stores and (opens_bank or stores[0][0] <= place < HOLD_STORES_FROM or place >= GRID * UNITS):
                chunk = stores[0][1]
                stores.remove(stores[0])
                first, done = chunk[0], chunk[-1] + 1
                if first // GROUP_TILES == ROW_TILES // GROUP_TILES:
                    add_and_store(first, len(chunk), tenth_base[first // GROUP_TILES], sums[first // GROUP_TILES])
                elif done % GROUP_TILES == 0:
                    add_and_store(done - GROUP_TILES, GROUP_TILES, tenth_base[first // GROUP_TILES], sums[first // GROUP_TILES])
            return spline_sums, basis

        for unit in range(UNITS):
            r, g = unit // GRID, unit % GRID
            chunk = chunk_of[r]
            first = chunk[0]

            if g == 0 and 1 <= r <= BANKS:
                x_t = transpose_x(r - 1)
            if g == 1 and r in TENTH_AT:
                group = TENTH_AT.index(r)
                tenth_base[group] = a_tenth_of(base_sums, min(GROUP_TILES, ROW_TILES - group * GROUP_TILES))
            gap_sq = gap_squared(turned[unit])
            if r >= SCALAR_CLAMPS_FROM:
                gap = clamped_gap(turned[unit])
            shifted_sq = shifted_squared(shifted[unit])
            if unit + AHEAD < UNITS:
                twice_dist[unit + AHEAD] = twice_distance(unit + AHEAD)
            if g == 1 and 1 <= r <= BANKS:
                if (r - 1) % BANKS_PER_GROUP == 0:
                    x_grouped = work.tile([P, BANKS_PER_GROUP * BANK_ROWS, PACK], BF16, align_bytes=64)
                regroup_x(r - 1, x_t, x_grouped)

            if r == first and g == 0:
                outer[first] = work.tile([P, len(chunk), GRID, TILE_X], BF16, name="outer")
                inner[first] = work.tile([P, len(chunk), GRID, TILE_X], BF16, name="inner")
            if r >= SCALAR_CLAMPS_FROM:
                outer_piece(outer[first][:, r - first, g, :], gap, gap_sq)
            else:
                minus_outer_piece(outer[first][:, r - first, g, :], turned[unit], gap_sq)
            if unit + AHEAD - 1 < UNITS:
                shifted[unit + AHEAD - 1] = transpose_and_shift(twice_dist[unit + AHEAD - 1])
            spline_sums, basis = one_step(place, spline_sums, basis)
            place += 1
            inner_piece(inner[first][:, r - first, g, :], shifted[unit], shifted_sq)
            if unit + AHEAD < UNITS:
                turned[unit + AHEAD] = transpose_plain(twice_dist[unit + AHEAD])
            spline_sums, basis = one_step(place, spline_sums, basis)
            place += 1
            if r == chunk[-1] and g == GRID - 1:
                if r < SCALAR_CLAMPS_FROM:
                    steps.append(("clamp", chunk))
                steps.extend([("choose", chunk), ("multiply", chunk)])
            if g == 1 and r in QUANTISE_X_AT:
                group = QUANTISE_X_AT.index(r)
                base_sums = base_product(x_grouped, min(GROUP_TILES, ROW_TILES - group * GROUP_TILES))
        while steps or stores:
            spline_sums, basis = one_step(place, spline_sums, basis)
            place += 1
